import numpy as np
import ml_dtypes


def mxq(x, axis, fmt="e4m3"):
    dtype, down = {"e4m3": (ml_dtypes.float8_e4m3fn, 7), "e5m2": (ml_dtypes.float8_e5m2, 14)}[fmt]
    v = np.moveaxis(np.asarray(x, np.float32).astype(ml_dtypes.bfloat16).astype(np.float64), axis, -1)
    blocks = v.reshape(v.shape[:-1] + (-1, 32))
    amax = np.abs(blocks).max(-1, keepdims=True)
    byte = np.maximum(np.where(amax > 0, np.frexp(amax)[1] - 1 + 127, 0) - down, 1)
    scale = np.exp2(byte - 127.0)
    codes = (blocks / scale).astype(np.float32).astype(dtype).astype(np.float64)
    return np.moveaxis((codes * scale).reshape(v.shape), -1, axis)


WIDE = False


def mx_kscale(k):
    if not WIDE:
        return np.ones(k)
    levels = np.array([10, -10, 5, -5, 0])
    a = np.random.permutation(np.resize(levels, k // 512 * 4)).reshape(k // 512, 4)
    idx = np.arange(k)
    return np.exp2(a[idx // 512, idx % 128 // 32])


BF16 = ml_dtypes.bfloat16


def bf(x):
    return np.asarray(x, np.float32).astype(BF16)


def f64(x):
    return np.asarray(x).astype(np.float64)


B, N, DI, D, H, DO = 8, 512, 1024, 512, 2, 256
DH = D // H
SCALE = np.sqrt(DH)
SIG = 0.5
VS = 0.1 * np.sqrt(N)


def time_concat(space):
    t = np.sqrt(1.0 + np.sum(space * space, axis=-1, keepdims=True))
    return np.concatenate([t, space], axis=-1)


def setup_inputs():
    t = mx_kscale(D)
    tq = np.sqrt(1.0 + SIG**2 * np.sum(np.random.standard_normal((B, H, N, DH)) ** 2, axis=-1))
    tk = np.sqrt(1.0 + SIG**2 * np.sum(np.random.standard_normal((B, H, N, DH)) ** 2, axis=-1))
    return {"qk_space": bf(np.random.standard_normal((B, H, N, N)) * SIG**2 * np.sqrt(DH)),
            "tq": bf(tq),
            "tk": bf(tk),
            "v_space": bf(np.random.standard_normal((B, H, N, DH)) * VS * t.reshape(H, 1, DH)),
            "Wo": bf(np.random.standard_normal((DO, D)) / np.sqrt(D) / t),
            "bo": bf(np.random.standard_normal(DO) * 0.05)}


def reference(qk_space, tq, tk, v_space, Wo, bo):
    inner = f64(qk_space) - f64(tq)[..., :, None] * f64(tk)[..., None, :]
    s = -inner / SCALE
    e = np.exp(s - s.max(-1, keepdims=True))
    z = (mxq(e, 3, "e4m3") @ mxq(f64(v_space), 2, "e4m3")) / e.sum(-1, keepdims=True)
    m = z.transpose(0, 2, 1, 3).reshape(B, N, D)
    y = (mxq(m, 2, "e4m3") @ mxq(f64(Wo), 1, "e4m3").T) + f64(bo)
    return time_concat(y)

@@ -1,0 +1,304 @@
+from contextlib import ExitStack
+
+import concourse.masks as masks
+import concourse.mybir as mybir
+
+F32 = mybir.dt.float32
+BF16 = mybir.dt.bfloat16
+U32 = mybir.dt.uint32
+U8 = mybir.dt.uint8
+FP8X4 = mybir.dt.float8_e4m3fn_x4
+ALU = mybir.AluOpType
+ACT = mybir.ActivationFunctionType
+
+P = 128
+PACK = 4
+BATCH, HEADS, SEQ, HEAD_DIM, OUT_DIM = 8, 2, 512, 256, 256
+MODEL_DIM = HEADS * HEAD_DIM
+ROW_TILES = SEQ // P
+PAIRS = ROW_TILES // 2
+UNITS = BATCH * HEADS * PAIRS
+TILES = BATCH * ROW_TILES
+INV_SCALE = 1.0 / 16.0
+
+LAG_SCORE = -1
+LAG_EXP = 0
+LAG_TRANSPOSE_E = 1
+LAG_REGROUP_E = 2
+LAG_QUANTISE_E = 3
+LAG_ATTEND = 4
+LAG_NORMALISE = 5
+LAG_TRANSPOSE_M = 8
+LAG_REGROUP_M = 9
+LAG_QUANTISE_M = 10
+LAG_PROJECT = 11
+LAG_BIAS = 12
+LAG_SQUARES = 13
+LAG_FINISH = 14
+
+FLOPS = 2 * BATCH * HEADS * SEQ * SEQ * HEAD_DIM + 2 * BATCH * SEQ * MODEL_DIM * OUT_DIM
+
+
+def transpose_rows(nc, psum, tag, identity, rows):
+    tiles = rows.shape[1]
+    bank = psum.tile([P, tiles, PACK, P], BF16, tag=tag)
+    for a in range(tiles):
+        for t in range(PACK):
+            nc.tensor.transpose(
+                out=bank[:, a, t, :], in_=rows[:, a, t * P : (t + 1) * P], identity=identity
+            )
+    return bank
+
+
+def regroup(nc, pool, bank, name):
+    tiles = bank[:].shape[1]
+    grouped = pool.tile([P, tiles, P, PACK], BF16, align_bytes=64, name=name)
+    nc.scalar.copy(out=grouped[:], in_=bank[:].rearrange("p a t r -> p a r t"))
+    return grouped
+
+
+def quantise(nc, pool, grouped, name):
+    words = grouped.shape[1] // PACK
+    codes = pool.tile([P, words], U32, align_bytes=64, name=name + "_codes")
+    scales = pool.tile([P, words], U8, align_bytes=64, name=name + "_scales")
+    nc.vector.quantize_mx(out=codes[:].bitcast(FP8X4), scales=scales[:], in_=grouped)
+    return codes, scales
+
+
+def multiply(nc, product, rows, tile_index, columns):
+    row_codes, row_scales = rows
+    column_codes, column_scales = columns
+    tile_columns = slice(tile_index * P, (tile_index + 1) * P)
+    nc.tensor.matmul_mx(
+        out=product,
+        lhsT=row_codes[:, tile_columns].bitcast(FP8X4),
+        lhsT_scale=row_scales[:, tile_columns],
+        rhs=column_codes[:].bitcast(FP8X4),
+        rhs_scale=column_scales[:],
+        start=True,
+        stop=True,
+    )
+
+
+def tile_lorentzmultiheadattention_pb_t_kernel(
+    tc, qk_space, tq, tk, v_space, Wo, bo, out
+):
+    nc = tc.nc
+    with ExitStack() as ctx:
+        ctx.enter_context(tc.manual_schedule())
+        const = ctx.enter_context(tc.tile_pool(name="const", bufs=1))
+        inputs = ctx.enter_context(tc.tile_pool(name="inputs", bufs=BATCH * HEADS))
+        work = ctx.enter_context(tc.tile_pool(name="work", bufs=3))
+        kept = ctx.enter_context(tc.tile_pool(name="kept", bufs=5))
+        psum = ctx.enter_context(tc.psum_pool(name="psum", bufs=2))
+
+        identity = const.tile([P, P], BF16)
+        masks.make_identity(nc, identity[:])
+        half = const.tile([P, 1], F32)
+        nc.gpsimd.memset(half[:], 0.5)
+
+        tq_rows = const.tile([P, P], BF16)
+        nc.vector.memset(tq_rows[64:128, :], 0.0)
+        nc.sync.dma_start(out=tq_rows[0:64, :], in_=tq.rearrange("b h (t p) -> (b h t) p", p=P))
+        wo_rows = const.tile([P, 2, MODEL_DIM], BF16)
+        bias = const.tile([P, OUT_DIM], BF16)
+        qk_tiles, v_tiles, tk_tiles = [], [], []
+        for n in range(BATCH * HEADS):
+            b, h = n // HEADS, n % HEADS
+            tk_all = inputs.tile([P, SEQ], BF16)
+            nc.gpsimd.dma_start(out=tk_all[:], in_=tk[b, h].partition_broadcast(P))
+            tk_tiles.append(tk_all)
+            qk_rows = inputs.tile([P, ROW_TILES, SEQ], BF16)
+            nc.sync.dma_start(
+                out=qk_rows[:], in_=qk_space[b, h].rearrange("(t p) j -> p t j", p=P)
+            )
+            qk_tiles.append(qk_rows)
+            if n == 0:
+                nc.sync.dma_start(out=wo_rows[:], in_=Wo.rearrange("(a p) k -> p a k", p=P))
+            v_rows = inputs.tile([P, PACK, HEAD_DIM], BF16)
+            nc.sync.dma_start(
+                out=v_rows[:], in_=v_space[b, h].rearrange("(t p) d -> p t d", p=P)
+            )
+            v_tiles.append(v_rows)
+            if n == 1:
+                nc.sync.dma_start(out=bias[:], in_=bo.partition_broadcast(P))
+
+        tq_bank = psum.tile([P, 2, PACK, P], BF16, tag="e_bank")
+        nc.tensor.transpose(out=tq_bank[:, 0, 0, :], in_=tq_rows[:], identity=identity[:])
+        tq_columns = const.tile([P, 64], F32)
+        nc.vector.tensor_copy(out=tq_columns[:], in_=tq_bank[:, 0, 0, 0:64])
+
+        v_grouped_of, v_mx_of = {}, {}
+        scores_of, top_of, shift_of, e_rows_of, rowsum_of = {}, {}, {}, {}, {}
+        e_bank_of, e_grouped_of, e_mx_of, inv_rowsum_of, z_of = {}, {}, {}, {}, {}
+        merged_of, m_bank_of, m_grouped_of, m_mx_of = {}, {}, {}, {}
+        y_of, result_of, norm_of = {}, {}, {}
+
+        def score_products(u):
+            n, pair = u // PAIRS, u % PAIRS
+            scores = work.tile([P, 2, SEQ], F32)
+            for a in range(2):
+                t = 2 * pair + a
+                nc.vector.scalar_tensor_tensor(
+                    out=scores[:, a, :],
+                    in0=tk_tiles[n][:],
+                    scalar=tq_columns[:, n * ROW_TILES + t : n * ROW_TILES + t + 1],
+                    in1=qk_tiles[n][:, t, :],
+                    op0=ALU.mult,
+                    op1=ALU.subtract,
+                )
+            scores_of[u] = scores
+
+        def score_maxima(u):
+            top = work.tile([P, 2], F32)
+            for a in range(2):
+                nc.vector.tensor_reduce(
+                    out=top[:, a : a + 1],
+                    in_=scores_of[u][:, a, :],
+                    axis=mybir.AxisListType.X,
+                    op=ALU.max,
+                )
+            top_of[u] = top
+
+        def score_shift(u):
+            shift = work.tile([P, 2], F32)
+            nc.vector.tensor_scalar_mul(out=shift[:], in0=top_of[u][:], scalar1=-INV_SCALE)
+            shift_of[u] = shift
+
+        def regroup_values(n):
+            v_grouped = work.tile([P, HEAD_DIM, PACK], BF16, align_bytes=64)
+            nc.vector.tensor_copy(
+                out=v_grouped[:].rearrange("p (c i) t -> p c t i", i=4),
+                in_=v_tiles[n][:].rearrange("p t (c i) -> p c t i", i=4),
+            )
+            v_grouped_of[n] = v_grouped
+
+        def quantise_values(n):
+            v_mx_of[n] = quantise(nc, kept, v_grouped_of[n][:].rearrange("p d t -> p (d t)"), "v")
+
+        def quantise_e(u):
+            e_mx_of[u] = quantise(
+                nc, work, e_grouped_of[u][:].rearrange("p a r t -> p (a r t)"), "e"
+            )
+
+        def invert_rowsum(u):
+            inv_rowsum = kept.tile([P, 2], F32)
+            nc.vector.reciprocal(out=inv_rowsum[:], in_=rowsum_of[u][:])
+            inv_rowsum_of[u] = inv_rowsum
+
+        def quantise_m(r):
+            m_mx_of[r] = quantise(
+                nc, work, m_grouped_of[r][:].rearrange("p a r t -> p (a r t)"), "m"
+            )
+
+        def add_bias(r):
+            result = kept.tile([P, 1 + OUT_DIM], F32)
+            nc.vector.memset(result[:, 0:1], 1.0)
+            nc.vector.tensor_tensor(
+                out=result[:, 1:], in0=y_of[r][:], in1=bias[:], op=ALU.add
+            )
+            result_of[r] = result
+
+        def finish(r):
+            result = result_of[r]
+            nc.gpsimd.tensor_tensor(
+                out=result[:, 0:1], in0=norm_of[r][:], in1=half[:], op=ALU.pow
+            )
+            b, t = r // ROW_TILES, r % ROW_TILES
+            nc.sync.dma_start(out=out[b, t * P : (t + 1) * P, :], in_=result[:])
+
+        def exponentiate(u):
+            e_rows = work.tile([P, 2, SEQ], BF16)
+            rowsum = kept.tile([P, 2], F32)
+            for a in range(2):
+                nc.scalar.activation(
+                    out=e_rows[:, a, :],
+                    in_=scores_of[u][:, a, :],
+                    func=ACT.Exp,
+                    bias=shift_of[u][:, a : a + 1],
+                    scale=INV_SCALE,
+                    accum_out=rowsum[:, a : a + 1],
+                )
+            e_rows_of[u], rowsum_of[u] = e_rows, rowsum
+
+        def regroup_e(u):
+            e_grouped_of[u] = regroup(nc, work, e_bank_of[u], "e_grouped")
+
+        def normalise(u):
+            h = (u // PAIRS) % HEADS
+            block = (u // (HEADS * PAIRS)) * PAIRS + u % PAIRS
+            if h == 0:
+                merged = kept.tile([P, 2, MODEL_DIM], BF16)
+                merged_of[block] = merged
+            for a in range(2):
+                nc.scalar.activation(
+                    out=merged_of[block][:, a, h * HEAD_DIM : (h + 1) * HEAD_DIM],
+                    in_=z_of[u][:, a, :],
+                    func=ACT.Copy,
+                    scale=inv_rowsum_of[u][:, a : a + 1],
+                )
+
+        def regroup_m(r):
+            m_grouped_of[r] = regroup(nc, work, m_bank_of[r], "m_grouped")
+
+        def sum_squares(r):
+            squares = work.tile([P, 1 + OUT_DIM], F32)
+            norm = work.tile([P, 1], F32)
+            nc.scalar.activation(
+                out=squares[:], in_=result_of[r][:], func=ACT.Square, accum_out=norm[:]
+            )
+            norm_of[r] = norm
+
+        def transpose_e(u):
+            e_bank_of[u] = transpose_rows(nc, psum, "e_bank", identity[:], e_rows_of[u][:])
+
+        def attend(u):
+            z_bank = psum.tile([P, 2, HEAD_DIM], F32, tag="z")
+            for a in range(2):
+                multiply(nc, z_bank[:, a, :], e_mx_of[u], a, v_mx_of[u // PAIRS])
+            z_of[u] = z_bank
+
+        def transpose_m(r):
+            rows = merged_of[r // 2][:, r % 2 : r % 2 + 1, :]
+            m_bank_of[r] = transpose_rows(nc, psum, "m_bank", identity[:], rows)
+
+        def project(r):
+            y_bank = psum.tile([P, OUT_DIM], F32, tag="y")
+            multiply(nc, y_bank[:], m_mx_of[r], 0, wo_mx)
+            y_of[r] = y_bank
+
+        def at(stage, index, count):
+            if 0 <= index < count:
+                stage(index)
+
+        wo_grouped = regroup(
+            nc, const, transpose_rows(nc, psum, "e_bank", identity[:], wo_rows[:]), "wo_grouped"
+        )
+
+        score_products(0)
+        score_maxima(0)
+        score_shift(0)
+        wo_mx = quantise(nc, const, wo_grouped[:].rearrange("p a r t -> p (a r t)"), "wo")
+
+        for step in range(UNITS + LAG_FINISH):
+            at(add_bias, step - LAG_BIAS, TILES)
+            at(score_products, step - LAG_SCORE, UNITS)
+            at(score_maxima, step - LAG_SCORE, UNITS)
+            at(quantise_e, step - LAG_QUANTISE_E, UNITS)
+            at(score_shift, step - LAG_SCORE, UNITS)
+            at(invert_rowsum, step - LAG_QUANTISE_E, UNITS)
+            at(quantise_m, step - LAG_QUANTISE_M, TILES)
+            if step % PAIRS == 0:
+                at(regroup_values, step // PAIRS, BATCH * HEADS)
+            else:
+                at(quantise_values, step // PAIRS, BATCH * HEADS)
+            at(exponentiate, step - LAG_EXP, UNITS)
+            at(regroup_e, step - LAG_REGROUP_E, UNITS)
+            at(normalise, step - LAG_NORMALISE, UNITS)
+            at(regroup_m, step - LAG_REGROUP_M, TILES)
+            at(sum_squares, step - LAG_SQUARES, TILES)
+            at(finish, step - LAG_FINISH, TILES)
+            at(transpose_e, step - LAG_TRANSPOSE_E, UNITS)
+            at(transpose_m, step - LAG_TRANSPOSE_M, TILES)
+            at(attend, step - LAG_ATTEND, UNITS)
+            at(project, step - LAG_PROJECT, TILES)

@@ -41,11 +41,12 @@ FLOPS = 2 * BATCH * HEADS * SEQ * SEQ * HEAD_DIM + 2 * BATCH * SEQ * MODEL_DIM *
 
 def transpose_rows(nc, psum, tag, identity, rows):
     tiles = rows.shape[1]
-    bank = psum.tile([P, tiles, PACK, P], BF16, tag=tag)
+    bank = psum.tile([P, tiles, 2, P], F32, tag=tag)
     for a in range(tiles):
-        for t in range(PACK):
+        words = rows[:, a, :].bitcast(F32)
+        for u in range(2):
             nc.tensor.transpose(
-                out=bank[:, a, t, :], in_=rows[:, a, t * P : (t + 1) * P], identity=identity
+                out=bank[:, a, u, :], in_=words[:, u : 2 * P : 2], identity=identity
             )
     return bank
 
@@ -53,7 +54,7 @@ def transpose_rows(nc, psum, tag, identity, rows):
 def regroup(nc, pool, bank, name):
     tiles = bank[:].shape[1]
     grouped = pool.tile([P, tiles, P, PACK], BF16, align_bytes=64, name=name)
-    nc.scalar.copy(out=grouped[:], in_=bank[:].rearrange("p a t r -> p a r t"))
+    nc.scalar.copy(out=grouped[:].bitcast(F32), in_=bank[:].rearrange("p a u r -> p a r u"))
     return grouped
 
 
@@ -92,8 +93,10 @@ def tile_lorentzmultiheadattention_pb_t_kernel(
         kept = ctx.enter_context(tc.tile_pool(name="kept", bufs=5))
         psum = ctx.enter_context(tc.psum_pool(name="psum", bufs=2))
 
-        identity = const.tile([P, P], BF16)
+        identity = const.tile([P, P], F32)
         masks.make_identity(nc, identity[:])
+        identity_bf16 = const.tile([P, P], BF16)
+        masks.make_identity(nc, identity_bf16[:])
         half = const.tile([P, 1], F32)
         nc.gpsimd.memset(half[:], 0.5)
 
@@ -117,16 +120,16 @@ def tile_lorentzmultiheadattention_pb_t_kernel(
                 nc.sync.dma_start(out=wo_rows[:], in_=Wo.rearrange("(a p) k -> p a k", p=P))
             v_rows = inputs.tile([P, PACK, HEAD_DIM], BF16)
             nc.sync.dma_start(
-                out=v_rows[:], in_=v_space[b, h].rearrange("(t p) d -> p t d", p=P)
+                out=v_rows[:], in_=v_space[b, h].rearrange("(p t) d -> p t d", t=PACK)
             )
             v_tiles.append(v_rows)
             if n == 1:
                 nc.sync.dma_start(out=bias[:], in_=bo.partition_broadcast(P))
 
-        tq_bank = psum.tile([P, 2, PACK, P], BF16, tag="e_bank")
-        nc.tensor.transpose(out=tq_bank[:, 0, 0, :], in_=tq_rows[:], identity=identity[:])
+        tq_bank = psum.tile([P, P], BF16, tag="y")
+        nc.tensor.transpose(out=tq_bank[:], in_=tq_rows[:], identity=identity_bf16[:])
         tq_columns = const.tile([P, 64], F32)
-        nc.vector.tensor_copy(out=tq_columns[:], in_=tq_bank[:, 0, 0, 0:64])
+        nc.vector.tensor_copy(out=tq_columns[:], in_=tq_bank[:, 0:64])
 
         v_grouped_of, v_mx_of = {}, {}
         scores_of, top_of, shift_of, e_rows_of, rowsum_of = {}, {}, {}, {}, {}

@@ -16,9 +16,11 @@ PACK = 4
 BATCH, HEADS, SEQ, HEAD_DIM, OUT_DIM = 8, 2, 512, 256, 256
 MODEL_DIM = HEADS * HEAD_DIM
 ROW_TILES = SEQ // P
-PAIRS = ROW_TILES // 2
-UNITS = BATCH * HEADS * PAIRS
-TILES = BATCH * ROW_TILES
+PAIR = 2
+BLOCKS_PER_BATCH = ROW_TILES // PAIR
+BLOCKS = BATCH * BLOCKS_PER_BATCH
+UNITS = BLOCKS * HEADS
+ALL_HEADS = BATCH * HEADS
 INV_SCALE = 1.0 / 16.0
 
 LAG_SCORE = -1
@@ -28,21 +30,20 @@ LAG_REGROUP_E = 2
 LAG_QUANTISE_E = 3
 LAG_ATTEND = 4
 LAG_NORMALISE = 5
-LAG_TRANSPOSE_M = 8
-LAG_REGROUP_M = 9
-LAG_QUANTISE_M = 10
-LAG_PROJECT = 11
-LAG_BIAS = 12
-LAG_SQUARES = 13
-LAG_FINISH = 14
+LAG_TRANSPOSE_M = 7
+LAG_REGROUP_M = 8
+LAG_QUANTISE_M = 9
+LAG_PROJECT = 10
+LAG_BIAS = 11
+LAG_SQUARES = 12
+LAG_FINISH = 13
 
 FLOPS = 2 * BATCH * HEADS * SEQ * SEQ * HEAD_DIM + 2 * BATCH * SEQ * MODEL_DIM * OUT_DIM
 
 
 def transpose_rows(nc, psum, tag, identity, rows):
-    tiles = rows.shape[1]
-    bank = psum.tile([P, tiles, 2, P], F32, tag=tag)
-    for a in range(tiles):
+    bank = psum.tile([P, PAIR, 2, P], F32, tag=tag)
+    for a in range(PAIR):
         words = rows[:, a, :].bitcast(F32)
         for u in range(2):
             nc.tensor.transpose(
@@ -52,8 +53,7 @@ def transpose_rows(nc, psum, tag, identity, rows):
 
 
 def regroup(nc, pool, bank, name):
-    tiles = bank[:].shape[1]
-    grouped = pool.tile([P, tiles, P, PACK], BF16, align_bytes=64, name=name)
+    grouped = pool.tile([P, PAIR, P, PACK], BF16, align_bytes=64, name=name)
     nc.scalar.copy(out=grouped[:].bitcast(F32), in_=bank[:].rearrange("p a u r -> p a r u"))
     return grouped
 
@@ -88,48 +88,73 @@ def tile_lorentzmultiheadattention_pb_t_kernel(
     with ExitStack() as ctx:
         ctx.enter_context(tc.manual_schedule())
         const = ctx.enter_context(tc.tile_pool(name="const", bufs=1))
-        inputs = ctx.enter_context(tc.tile_pool(name="inputs", bufs=BATCH * HEADS))
+        inputs = ctx.enter_context(tc.tile_pool(name="inputs", bufs=ALL_HEADS))
         work = ctx.enter_context(tc.tile_pool(name="work", bufs=3))
         kept = ctx.enter_context(tc.tile_pool(name="kept", bufs=5))
         psum = ctx.enter_context(tc.psum_pool(name="psum", bufs=2))
 
-        identity = const.tile([P, P], F32)
-        masks.make_identity(nc, identity[:])
+        tq_rows = const.tile([P, SEQ], BF16)
+        nc.gpsimd.memset(tq_rows[:], 0.0)
         identity_bf16 = const.tile([P, P], BF16)
         masks.make_identity(nc, identity_bf16[:])
-        half = const.tile([P, 1], F32)
+        identity = const.tile([P, P], F32)
+        masks.make_identity(nc, identity[:])
+        half = const.tile([P, ROW_TILES], F32)
         nc.gpsimd.memset(half[:], 0.5)
 
-        tq_rows = const.tile([P, P], BF16)
-        nc.vector.memset(tq_rows[64:128, :], 0.0)
-        nc.sync.dma_start(out=tq_rows[0:64, :], in_=tq.rearrange("b h (t p) -> (b h t) p", p=P))
+        qk_tiles, v_tiles, tk_tiles = [], [], []
         wo_rows = const.tile([P, 2, MODEL_DIM], BF16)
         bias = const.tile([P, OUT_DIM], BF16)
-        qk_tiles, v_tiles, tk_tiles = [], [], []
-        for n in range(BATCH * HEADS):
-            b, h = n // HEADS, n % HEADS
-            tk_all = inputs.tile([P, SEQ], BF16)
-            nc.gpsimd.dma_start(out=tk_all[:], in_=tk[b, h].partition_broadcast(P))
+
+        def load_tk(b):
+            tk_all = inputs.tile([P, HEADS, SEQ], BF16)
+            nc.sync.dma_start(out=tk_all[:], in_=tk[b].partition_broadcast(P))
             tk_tiles.append(tk_all)
+
+        def load_qk(n):
             qk_rows = inputs.tile([P, ROW_TILES, SEQ], BF16)
-            nc.sync.dma_start(
-                out=qk_rows[:], in_=qk_space[b, h].rearrange("(t p) j -> p t j", p=P)
-            )
             qk_tiles.append(qk_rows)
-            if n == 0:
-                nc.sync.dma_start(out=wo_rows[:], in_=Wo.rearrange("(a p) k -> p a k", p=P))
+            return qk_space[n // HEADS, n % HEADS].rearrange("(p t) j -> p t j", t=ROW_TILES)
+
+        def load_v(n):
             v_rows = inputs.tile([P, PACK, HEAD_DIM], BF16)
             nc.sync.dma_start(
-                out=v_rows[:], in_=v_space[b, h].rearrange("(p t) d -> p t d", t=PACK)
+                out=v_rows[:],
+                in_=v_space[n // HEADS, n % HEADS].rearrange("(p t) d -> p t d", t=PACK),
             )
             v_tiles.append(v_rows)
-            if n == 1:
-                nc.sync.dma_start(out=bias[:], in_=bo.partition_broadcast(P))
 
-        tq_bank = psum.tile([P, P], BF16, tag="y")
-        nc.tensor.transpose(out=tq_bank[:], in_=tq_rows[:], identity=identity_bf16[:])
-        tq_columns = const.tile([P, 64], F32)
-        nc.vector.tensor_copy(out=tq_columns[:], in_=tq_bank[:, 0:64])
+        load_tk(0)
+        first_qk = [load_qk(h) for h in range(HEADS)]
+        for pair in range(BLOCKS_PER_BATCH):
+            tiles = slice(pair * PAIR, (pair + 1) * PAIR)
+            for h in range(HEADS):
+                nc.sync.dma_start(out=qk_tiles[h][:, tiles, :], in_=first_qk[h][:, tiles, :])
+                if pair == 0 and h == 0:
+                    nc.sync.dma_start(
+                        out=tq_rows[0:ALL_HEADS, :], in_=tq.rearrange("b h i -> (b h) i")
+                    )
+            if pair == 0:
+                nc.sync.dma_start(out=wo_rows[:], in_=Wo.rearrange("(a p) k -> p a k", p=P))
+                for h in range(HEADS):
+                    load_v(h)
+        nc.sync.dma_start(out=bias[:], in_=bo.partition_broadcast(P))
+        for b in range(1, BATCH):
+            load_tk(b)
+            for h in range(HEADS):
+                n = b * HEADS + h
+                qk_rows_hbm = load_qk(n)
+                nc.sync.dma_start(out=qk_tiles[n][:], in_=qk_rows_hbm)
+            for h in range(HEADS):
+                load_v(b * HEADS + h)
+
+        tq_bank = psum.tile([P, ROW_TILES, P], BF16, tag="y")
+        for t in range(ROW_TILES):
+            nc.tensor.transpose(
+                out=tq_bank[:, t, :], in_=tq_rows[:, t:SEQ:ROW_TILES], identity=identity_bf16[:]
+            )
+        tq_columns = const.tile([P, ROW_TILES, ALL_HEADS], F32)
+        nc.vector.tensor_copy(out=tq_columns[:], in_=tq_bank[:, :, 0:ALL_HEADS])
 
         v_grouped_of, v_mx_of = {}, {}
         scores_of, top_of, shift_of, e_rows_of, rowsum_of = {}, {}, {}, {}, {}
@@ -137,24 +162,28 @@ def tile_lorentzmultiheadattention_pb_t_kernel(
         merged_of, m_bank_of, m_grouped_of, m_mx_of = {}, {}, {}, {}
         y_of, result_of, norm_of = {}, {}, {}
 
+        def place(u):
+            c, h = u // HEADS, u % HEADS
+            b, pair = c // BLOCKS_PER_BATCH, c % BLOCKS_PER_BATCH
+            return b * HEADS + h, pair * PAIR
+
         def score_products(u):
-            n, pair = u // PAIRS, u % PAIRS
-            scores = work.tile([P, 2, SEQ], F32)
-            for a in range(2):
-                t = 2 * pair + a
+            n, first = place(u)
+            scores = work.tile([P, PAIR, SEQ], F32)
+            for a in range(PAIR):
                 nc.vector.scalar_tensor_tensor(
                     out=scores[:, a, :],
-                    in0=tk_tiles[n][:],
-                    scalar=tq_columns[:, n * ROW_TILES + t : n * ROW_TILES + t + 1],
-                    in1=qk_tiles[n][:, t, :],
+                    in0=tk_tiles[n // HEADS][:, n % HEADS, :],
+                    scalar=tq_columns[:, first + a, n : n + 1],
+                    in1=qk_tiles[n][:, first + a, :],
                     op0=ALU.mult,
                     op1=ALU.subtract,
                 )
             scores_of[u] = scores
 
         def score_maxima(u):
-            top = work.tile([P, 2], F32)
-            for a in range(2):
+            top = work.tile([P, PAIR], F32)
+            for a in range(PAIR):
                 nc.vector.tensor_reduce(
                     out=top[:, a : a + 1],
                     in_=scores_of[u][:, a, :],
@@ -164,7 +193,7 @@ def tile_lorentzmultiheadattention_pb_t_kernel(
             top_of[u] = top
 
         def score_shift(u):
-            shift = work.tile([P, 2], F32)
+            shift = work.tile([P, PAIR], F32)
             nc.vector.tensor_scalar_mul(out=shift[:], in0=top_of[u][:], scalar1=-INV_SCALE)
             shift_of[u] = shift
 
@@ -185,35 +214,47 @@ def tile_lorentzmultiheadattention_pb_t_kernel(
             )
 
         def invert_rowsum(u):
-            inv_rowsum = kept.tile([P, 2], F32)
+            inv_rowsum = kept.tile([P, PAIR], F32)
             nc.vector.reciprocal(out=inv_rowsum[:], in_=rowsum_of[u][:])
             inv_rowsum_of[u] = inv_rowsum
 
-        def quantise_m(r):
-            m_mx_of[r] = quantise(
-                nc, work, m_grouped_of[r][:].rearrange("p a r t -> p (a r t)"), "m"
+        def quantise_m(c):
+            m_mx_of[c] = quantise(
+                nc, work, m_grouped_of[c][:].rearrange("p a r t -> p (a r t)"), "m"
             )
 
-        def add_bias(r):
-            result = kept.tile([P, 1 + OUT_DIM], F32)
-            nc.vector.memset(result[:, 0:1], 1.0)
+        def add_bias(c):
+            b, pair = c // BLOCKS_PER_BATCH, c % BLOCKS_PER_BATCH
+            if pair == 0:
+                result = work.tile([P, ROW_TILES, 1 + OUT_DIM], F32)
+                result_of[b] = result
             nc.vector.tensor_tensor(
-                out=result[:, 1:], in0=y_of[r][:], in1=bias[:], op=ALU.add
+                out=result_of[b][:, pair * PAIR : (pair + 1) * PAIR, 1:],
+                in0=y_of[c][:],
+                in1=bias[:].unsqueeze(1).to_broadcast([P, PAIR, OUT_DIM]),
+                op=ALU.add,
             )
-            result_of[r] = result
 
-        def finish(r):
-            result = result_of[r]
-            nc.gpsimd.tensor_tensor(
-                out=result[:, 0:1], in0=norm_of[r][:], in1=half[:], op=ALU.pow
+        def finish(c):
+            b, pair = c // BLOCKS_PER_BATCH, c % BLOCKS_PER_BATCH
+            tiles = slice(pair * PAIR, (pair + 1) * PAIR)
+            radicand = work.tile([P, PAIR], F32)
+            nc.gpsimd.tensor_scalar(
+                out=radicand[:], in0=norm_of[c][:], scalar1=1.0, scalar2=None, op0=ALU.add
             )
-            b, t = r // ROW_TILES, r % ROW_TILES
-            nc.sync.dma_start(out=out[b, t * P : (t + 1) * P, :], in_=result[:])
+            nc.gpsimd.tensor_tensor(
+                out=result_of[b][:, tiles, 0],
+                in0=radicand[:],
+                in1=half[:, 0:PAIR],
+                op=ALU.pow,
+            )
+            rows = out[b].rearrange("(p t) o -> p t o", t=ROW_TILES)
+            nc.sync.dma_start(out=rows[:, tiles, :], in_=result_of[b][:, tiles, :])
 
         def exponentiate(u):
-            e_rows = work.tile([P, 2, SEQ], BF16)
-            rowsum = kept.tile([P, 2], F32)
-            for a in range(2):
+            e_rows = work.tile([P, PAIR, SEQ], BF16)
+            rowsum = kept.tile([P, PAIR], F32)
+            for a in range(PAIR):
                 nc.scalar.activation(
                     out=e_rows[:, a, :],
                     in_=scores_of[u][:, a, :],
@@ -228,51 +269,60 @@ def tile_lorentzmultiheadattention_pb_t_kernel(
             e_grouped_of[u] = regroup(nc, work, e_bank_of[u], "e_grouped")
 
         def normalise(u):
-            h = (u // PAIRS) % HEADS
-            block = (u // (HEADS * PAIRS)) * PAIRS + u % PAIRS
+            c, h = u // HEADS, u % HEADS
             if h == 0:
-                merged = kept.tile([P, 2, MODEL_DIM], BF16)
-                merged_of[block] = merged
-            for a in range(2):
+                merged = work.tile([P, PAIR, MODEL_DIM], BF16)
+                merged_of[c] = merged
+            for a in range(PAIR):
                 nc.scalar.activation(
-                    out=merged_of[block][:, a, h * HEAD_DIM : (h + 1) * HEAD_DIM],
+                    out=merged_of[c][:, a, h * HEAD_DIM : (h + 1) * HEAD_DIM],
                     in_=z_of[u][:, a, :],
                     func=ACT.Copy,
                     scale=inv_rowsum_of[u][:, a : a + 1],
                 )
 
-        def regroup_m(r):
-            m_grouped_of[r] = regroup(nc, work, m_bank_of[r], "m_grouped")
+        def regroup_m(c):
+            m_grouped_of[c] = regroup(nc, work, m_bank_of[c], "m_grouped")
 
-        def sum_squares(r):
-            squares = work.tile([P, 1 + OUT_DIM], F32)
-            norm = work.tile([P, 1], F32)
-            nc.scalar.activation(
-                out=squares[:], in_=result_of[r][:], func=ACT.Square, accum_out=norm[:]
-            )
-            norm_of[r] = norm
+        def sum_squares(c):
+            b, pair = c // BLOCKS_PER_BATCH, c % BLOCKS_PER_BATCH
+            squares = work.tile([P, OUT_DIM], F32)
+            norm = work.tile([P, PAIR], F32)
+            for a in range(PAIR):
+                nc.scalar.activation(
+                    out=squares[:],
+                    in_=result_of[b][:, pair * PAIR + a, 1:],
+                    func=ACT.Square,
+                    accum_out=norm[:, a : a + 1],
+                )
+            norm_of[c] = norm
 
         def transpose_e(u):
             e_bank_of[u] = transpose_rows(nc, psum, "e_bank", identity[:], e_rows_of[u][:])
 
         def attend(u):
-            z_bank = psum.tile([P, 2, HEAD_DIM], F32, tag="z")
-            for a in range(2):
-                multiply(nc, z_bank[:, a, :], e_mx_of[u], a, v_mx_of[u // PAIRS])
+            n, first = place(u)
+            z_bank = psum.tile([P, PAIR, HEAD_DIM], F32, tag="z")
+            for a in range(PAIR):
+                multiply(nc, z_bank[:, a, :], e_mx_of[u], a, v_mx_of[n])
             z_of[u] = z_bank
 
-        def transpose_m(r):
-            rows = merged_of[r // 2][:, r % 2 : r % 2 + 1, :]
-            m_bank_of[r] = transpose_rows(nc, psum, "m_bank", identity[:], rows)
+        def transpose_m(c):
+            m_bank_of[c] = transpose_rows(nc, psum, "m_bank", identity[:], merged_of[c][:])
 
-        def project(r):
-            y_bank = psum.tile([P, OUT_DIM], F32, tag="y")
-            multiply(nc, y_bank[:], m_mx_of[r], 0, wo_mx)
-            y_of[r] = y_bank
+        def project(c):
+            y_bank = psum.tile([P, PAIR, OUT_DIM], F32, tag="y")
+            for a in range(PAIR):
+                multiply(nc, y_bank[:, a, :], m_mx_of[c], a, wo_mx)
+            y_of[c] = y_bank
 
         def at(stage, index, count):
             if 0 <= index < count:
                 stage(index)
+
+        def at_block(stage, index):
+            if index % HEADS == 0:
+                at(stage, index // HEADS, BLOCKS)
 
         wo_grouped = regroup(
             nc, const, transpose_rows(nc, psum, "e_bank", identity[:], wo_rows[:]), "wo_grouped"
@@ -284,24 +334,24 @@ def tile_lorentzmultiheadattention_pb_t_kernel(
         wo_mx = quantise(nc, const, wo_grouped[:].rearrange("p a r t -> p (a r t)"), "wo")
 
         for step in range(UNITS + LAG_FINISH):
-            at(add_bias, step - LAG_BIAS, TILES)
+            at_block(add_bias, step - LAG_BIAS)
             at(score_products, step - LAG_SCORE, UNITS)
             at(score_maxima, step - LAG_SCORE, UNITS)
             at(quantise_e, step - LAG_QUANTISE_E, UNITS)
             at(score_shift, step - LAG_SCORE, UNITS)
             at(invert_rowsum, step - LAG_QUANTISE_E, UNITS)
-            at(quantise_m, step - LAG_QUANTISE_M, TILES)
-            if step % PAIRS == 0:
-                at(regroup_values, step // PAIRS, BATCH * HEADS)
+            at_block(quantise_m, step - LAG_QUANTISE_M)
+            if step % 2 == 0:
+                at(regroup_values, step // 2, ALL_HEADS)
             else:
-                at(quantise_values, step // PAIRS, BATCH * HEADS)
+                at(quantise_values, step // 2, ALL_HEADS)
             at(exponentiate, step - LAG_EXP, UNITS)
             at(regroup_e, step - LAG_REGROUP_E, UNITS)
             at(normalise, step - LAG_NORMALISE, UNITS)
-            at(regroup_m, step - LAG_REGROUP_M, TILES)
-            at(sum_squares, step - LAG_SQUARES, TILES)
-            at(finish, step - LAG_FINISH, TILES)
+            at_block(regroup_m, step - LAG_REGROUP_M)
+            at_block(sum_squares, step - LAG_SQUARES)
+            at_block(finish, step - LAG_FINISH)
             at(transpose_e, step - LAG_TRANSPOSE_E, UNITS)
-            at(transpose_m, step - LAG_TRANSPOSE_M, TILES)
+            at_block(transpose_m, step - LAG_TRANSPOSE_M)
             at(attend, step - LAG_ATTEND, UNITS)
-            at(project, step - LAG_PROJECT, TILES)
+            at_block(project, step - LAG_PROJECT)

@@ -18,6 +18,7 @@ MODEL_DIM = HEADS * HEAD_DIM
 ROW_TILES = SEQ // P
 PAIR = 2
 BLOCKS_PER_BATCH = ROW_TILES // PAIR
+GROUP_TILES = 2 * ROW_TILES
 BLOCKS = BATCH * BLOCKS_PER_BATCH
 UNITS = BLOCKS * HEADS
 ALL_HEADS = BATCH * HEADS
@@ -91,6 +92,7 @@ def tile_lorentzmultiheadattention_pb_t_kernel(
         inputs = ctx.enter_context(tc.tile_pool(name="inputs", bufs=ALL_HEADS))
         work = ctx.enter_context(tc.tile_pool(name="work", bufs=3))
         kept = ctx.enter_context(tc.tile_pool(name="kept", bufs=5))
+        groups = ctx.enter_context(tc.tile_pool(name="groups", bufs=2))
         psum = ctx.enter_context(tc.psum_pool(name="psum", bufs=2))
 
         tq_rows = const.tile([P, SEQ], BF16)
@@ -99,7 +101,7 @@ def tile_lorentzmultiheadattention_pb_t_kernel(
         masks.make_identity(nc, identity_bf16[:])
         identity = const.tile([P, P], F32)
         masks.make_identity(nc, identity[:])
-        half = const.tile([P, ROW_TILES], F32)
+        half = const.tile([P, GROUP_TILES], F32)
         nc.gpsimd.memset(half[:], 0.5)
 
         qk_tiles, v_tiles, tk_tiles = [], [], []
@@ -167,6 +169,9 @@ def tile_lorentzmultiheadattention_pb_t_kernel(
             b, pair = c // BLOCKS_PER_BATCH, c % BLOCKS_PER_BATCH
             return b * HEADS + h, pair * PAIR
 
+        def group_place(c):
+            return divmod(c * PAIR, GROUP_TILES)
+
         def score_products(u):
             n, first = place(u)
             scores = work.tile([P, PAIR, SEQ], F32)
@@ -224,32 +229,50 @@ def tile_lorentzmultiheadattention_pb_t_kernel(
             )
 
         def add_bias(c):
-            b, pair = c // BLOCKS_PER_BATCH, c % BLOCKS_PER_BATCH
-            if pair == 0:
-                result = work.tile([P, ROW_TILES, 1 + OUT_DIM], F32)
-                result_of[b] = result
+            group, first = group_place(c)
+            if first == 0:
+                result = groups.tile([P, GROUP_TILES, 1 + OUT_DIM], F32)
+                norm = groups.tile([P, GROUP_TILES], F32)
+                result_of[group], norm_of[group] = result, norm
             nc.vector.tensor_tensor(
-                out=result_of[b][:, pair * PAIR : (pair + 1) * PAIR, 1:],
+                out=result_of[group][:, first : first + PAIR, 1:],
                 in0=y_of[c][:],
                 in1=bias[:].unsqueeze(1).to_broadcast([P, PAIR, OUT_DIM]),
                 op=ALU.add,
             )
 
         def finish(c):
-            b, pair = c // BLOCKS_PER_BATCH, c % BLOCKS_PER_BATCH
-            tiles = slice(pair * PAIR, (pair + 1) * PAIR)
-            radicand = work.tile([P, PAIR], F32)
+            group, first = group_place(c)
+            if c < BLOCKS - GROUP_TILES // PAIR:
+                if first + PAIR < GROUP_TILES:
+                    return
+                tiles = range(0, GROUP_TILES)
+            else:
+                tiles = range(first, first + PAIR)
+            span = slice(tiles[0], tiles[-1] + 1)
+            radicand = groups.tile([P, GROUP_TILES], F32)
             nc.gpsimd.tensor_scalar(
-                out=radicand[:], in0=norm_of[c][:], scalar1=1.0, scalar2=None, op0=ALU.add
+                out=radicand[:, span],
+                in0=norm_of[group][:, span],
+                scalar1=1.0,
+                scalar2=None,
+                op0=ALU.add,
             )
             nc.gpsimd.tensor_tensor(
-                out=result_of[b][:, tiles, 0],
-                in0=radicand[:],
-                in1=half[:, 0:PAIR],
+                out=result_of[group][:, span, 0],
+                in0=radicand[:, span],
+                in1=half[:, span],
                 op=ALU.pow,
             )
-            rows = out[b].rearrange("(p t) o -> p t o", t=ROW_TILES)
-            nc.sync.dma_start(out=rows[:, tiles, :], in_=result_of[b][:, tiles, :])
+            store_tiles = min(len(tiles), ROW_TILES)
+            for start in range(tiles[0], tiles[-1] + 1, store_tiles):
+                b = group * (GROUP_TILES // ROW_TILES) + start // ROW_TILES
+                t = start % ROW_TILES
+                rows = out[b].rearrange("(p t) o -> p t o", t=ROW_TILES)
+                nc.sync.dma_start(
+                    out=rows[:, t : t + store_tiles, :],
+                    in_=result_of[group][:, start : start + store_tiles, :],
+                )
 
         def exponentiate(u):
             e_rows = work.tile([P, PAIR, SEQ], BF16)
@@ -285,17 +308,15 @@ def tile_lorentzmultiheadattention_pb_t_kernel(
             m_grouped_of[c] = regroup(nc, work, m_bank_of[c], "m_grouped")
 
         def sum_squares(c):
-            b, pair = c // BLOCKS_PER_BATCH, c % BLOCKS_PER_BATCH
+            group, first = group_place(c)
             squares = work.tile([P, OUT_DIM], F32)
-            norm = work.tile([P, PAIR], F32)
-            for a in range(PAIR):
+            for t in range(first, first + PAIR):
                 nc.scalar.activation(
                     out=squares[:],
-                    in_=result_of[b][:, pair * PAIR + a, 1:],
+                    in_=result_of[group][:, t, 1:],
                     func=ACT.Square,
-                    accum_out=norm[:, a : a + 1],
+                    accum_out=norm_of[group][:, t : t + 1],
                 )
-            norm_of[c] = norm
 
         def transpose_e(u):
             e_bank_of[u] = transpose_rows(nc, psum, "e_bank", identity[:], e_rows_of[u][:])

@@ -22,8 +22,11 @@ GROUP_TILES = 2 * ROW_TILES
 BLOCKS = BATCH * BLOCKS_PER_BATCH
 UNITS = BLOCKS * HEADS
 ALL_HEADS = BATCH * HEADS
+SCALAR_HEADS = 8
 INV_SCALE = 1.0 / 16.0
+TENSOR_SCORED = range(7, UNITS, 8)
 
+LAG_SCORE_ON_TENSOR = -2
 LAG_SCORE = -1
 LAG_EXP = 0
 LAG_TRANSPOSE_E = 1
@@ -42,8 +45,8 @@ LAG_FINISH = 13
 FLOPS = 2 * BATCH * HEADS * SEQ * SEQ * HEAD_DIM + 2 * BATCH * SEQ * MODEL_DIM * OUT_DIM
 
 
-def transpose_rows(nc, psum, tag, identity, rows):
-    bank = psum.tile([P, PAIR, 2, P], F32, tag=tag)
+def transpose_rows(nc, psum, tag, bufs, identity, rows):
+    bank = psum.tile([P, PAIR, 2, P], F32, tag=tag, bufs=bufs)
     for a in range(PAIR):
         words = rows[:, a, :].bitcast(F32)
         for u in range(2):
@@ -95,12 +98,19 @@ def tile_lorentzmultiheadattention_pb_t_kernel(
         groups = ctx.enter_context(tc.tile_pool(name="groups", bufs=2))
         psum = ctx.enter_context(tc.psum_pool(name="psum", bufs=2))
 
+        def place(u):
+            c, h = u // HEADS, u % HEADS
+            b, pair = c // BLOCKS_PER_BATCH, c % BLOCKS_PER_BATCH
+            return b * HEADS + h, pair * PAIR
+
         tq_rows = const.tile([P, SEQ], BF16)
-        nc.gpsimd.memset(tq_rows[:], 0.0)
+        nc.vector.memset(tq_rows[:], 0.0)
         identity_bf16 = const.tile([P, P], BF16)
         masks.make_identity(nc, identity_bf16[:])
         identity = const.tile([P, P], F32)
         masks.make_identity(nc, identity[:])
+        minus_identity = const.tile([P, P], BF16)
+        nc.vector.tensor_scalar_mul(out=minus_identity[:], in0=identity_bf16[:], scalar1=-1.0)
         half = const.tile([P, GROUP_TILES], F32)
         nc.gpsimd.memset(half[:], 0.5)
 
@@ -141,6 +151,15 @@ def tile_lorentzmultiheadattention_pb_t_kernel(
                 for h in range(HEADS):
                     load_v(h)
         nc.sync.dma_start(out=bias[:], in_=bo.partition_broadcast(P))
+        tk_row_of = {}
+        for u in TENSOR_SCORED:
+            n = place(u)[0]
+            tk_row = const.tile([P, SEQ], BF16, name="tk_row_" + str(u))
+            nc.vector.memset(tk_row[:], 0.0)
+            nc.sync.dma_start(
+                out=tk_row[n : n + 1, :], in_=tk[n // HEADS, n % HEADS : n % HEADS + 1]
+            )
+            tk_row_of[u] = tk_row
         for b in range(1, BATCH):
             load_tk(b)
             for h in range(HEADS):
@@ -150,7 +169,7 @@ def tile_lorentzmultiheadattention_pb_t_kernel(
             for h in range(HEADS):
                 load_v(b * HEADS + h)
 
-        tq_bank = psum.tile([P, ROW_TILES, P], BF16, tag="y")
+        tq_bank = psum.tile([P, ROW_TILES, P], BF16, tag="y", bufs=1)
         for t in range(ROW_TILES):
             nc.tensor.transpose(
                 out=tq_bank[:, t, :], in_=tq_rows[:, t:SEQ:ROW_TILES], identity=identity_bf16[:]
@@ -164,15 +183,12 @@ def tile_lorentzmultiheadattention_pb_t_kernel(
         merged_of, m_bank_of, m_grouped_of, m_mx_of = {}, {}, {}, {}
         y_of, result_of, norm_of = {}, {}, {}
 
-        def place(u):
-            c, h = u // HEADS, u % HEADS
-            b, pair = c // BLOCKS_PER_BATCH, c % BLOCKS_PER_BATCH
-            return b * HEADS + h, pair * PAIR
-
         def group_place(c):
             return divmod(c * PAIR, GROUP_TILES)
 
         def score_products(u):
+            if u in TENSOR_SCORED:
+                return
             n, first = place(u)
             scores = work.tile([P, PAIR, SEQ], F32)
             for a in range(PAIR):
@@ -184,14 +200,14 @@ def tile_lorentzmultiheadattention_pb_t_kernel(
                     op0=ALU.mult,
                     op1=ALU.subtract,
                 )
-            scores_of[u] = scores
+            scores_of[u] = [scores[:, a, :] for a in range(PAIR)]
 
         def score_maxima(u):
             top = work.tile([P, PAIR], F32)
             for a in range(PAIR):
                 nc.vector.tensor_reduce(
                     out=top[:, a : a + 1],
-                    in_=scores_of[u][:, a, :],
+                    in_=scores_of[u][a],
                     axis=mybir.AxisListType.X,
                     op=ALU.max,
                 )
@@ -204,14 +220,15 @@ def tile_lorentzmultiheadattention_pb_t_kernel(
 
         def regroup_values(n):
             v_grouped = work.tile([P, HEAD_DIM, PACK], BF16, align_bytes=64)
-            nc.vector.tensor_copy(
+            copy = nc.scalar.copy if n < SCALAR_HEADS else nc.vector.tensor_copy
+            copy(
                 out=v_grouped[:].rearrange("p (c i) t -> p c t i", i=4),
                 in_=v_tiles[n][:].rearrange("p t (c i) -> p c t i", i=4),
             )
             v_grouped_of[n] = v_grouped
 
         def quantise_values(n):
-            v_mx_of[n] = quantise(nc, kept, v_grouped_of[n][:].rearrange("p d t -> p (d t)"), "v")
+            v_mx_of[n] = quantise(nc, inputs, v_grouped_of[n][:].rearrange("p d t -> p (d t)"), "v")
 
         def quantise_e(u):
             e_mx_of[u] = quantise(
@@ -280,7 +297,7 @@ def tile_lorentzmultiheadattention_pb_t_kernel(
             for a in range(PAIR):
                 nc.scalar.activation(
                     out=e_rows[:, a, :],
-                    in_=scores_of[u][:, a, :],
+                    in_=scores_of[u][a],
                     func=ACT.Exp,
                     bias=shift_of[u][:, a : a + 1],
                     scale=INV_SCALE,
@@ -318,8 +335,31 @@ def tile_lorentzmultiheadattention_pb_t_kernel(
                     accum_out=norm_of[group][:, t : t + 1],
                 )
 
+        def score_on_tensor(u):
+            if u not in TENSOR_SCORED:
+                return
+            n, first = place(u)
+            scores_of[u] = []
+            for t in range(first, first + PAIR):
+                scores_bank = psum.tile([P, SEQ], F32, tag="scores", bufs=2)
+                nc.tensor.matmul(
+                    out=scores_bank[:],
+                    lhsT=minus_identity[:],
+                    rhs=qk_tiles[n][:, t, :],
+                    start=True,
+                    stop=False,
+                )
+                nc.tensor.matmul(
+                    out=scores_bank[:],
+                    lhsT=tq_rows[:, t:SEQ:ROW_TILES],
+                    rhs=tk_row_of[u][:],
+                    start=False,
+                    stop=True,
+                )
+                scores_of[u].append(scores_bank[:])
+
         def transpose_e(u):
-            e_bank_of[u] = transpose_rows(nc, psum, "e_bank", identity[:], e_rows_of[u][:])
+            e_bank_of[u] = transpose_rows(nc, psum, "e_bank", 2, identity[:], e_rows_of[u][:])
 
         def attend(u):
             n, first = place(u)
@@ -329,10 +369,12 @@ def tile_lorentzmultiheadattention_pb_t_kernel(
             z_of[u] = z_bank
 
         def transpose_m(c):
-            m_bank_of[c] = transpose_rows(nc, psum, "m_bank", identity[:], merged_of[c][:])
+            m_bank_of[c] = transpose_rows(
+                nc, psum, "m_bank", 1, identity[:], merged_of[c][:]
+            )
 
         def project(c):
-            y_bank = psum.tile([P, PAIR, OUT_DIM], F32, tag="y")
+            y_bank = psum.tile([P, PAIR, OUT_DIM], F32, tag="y", bufs=1)
             for a in range(PAIR):
                 multiply(nc, y_bank[:, a, :], m_mx_of[c], a, wo_mx)
             y_of[c] = y_bank
@@ -346,7 +388,7 @@ def tile_lorentzmultiheadattention_pb_t_kernel(
                 at(stage, index // HEADS, BLOCKS)
 
         wo_grouped = regroup(
-            nc, const, transpose_rows(nc, psum, "e_bank", identity[:], wo_rows[:]), "wo_grouped"
+            nc, const, transpose_rows(nc, psum, "e_bank", 2, identity[:], wo_rows[:]), "wo_grouped"
         )
 
         score_products(0)
@@ -362,11 +404,14 @@ def tile_lorentzmultiheadattention_pb_t_kernel(
             at(score_shift, step - LAG_SCORE, UNITS)
             at(invert_rowsum, step - LAG_QUANTISE_E, UNITS)
             at_block(quantise_m, step - LAG_QUANTISE_M)
-            if step % 2 == 0:
-                at(regroup_values, step // 2, ALL_HEADS)
-            else:
-                at(quantise_values, step // 2, ALL_HEADS)
+            at(quantise_values, step - 1, SCALAR_HEADS)
+            if step // 2 >= SCALAR_HEADS:
+                if step % 2 == 0:
+                    at(regroup_values, step // 2, ALL_HEADS)
+                else:
+                    at(quantise_values, step // 2, ALL_HEADS)
             at(exponentiate, step - LAG_EXP, UNITS)
+            at(regroup_values, step, SCALAR_HEADS)
             at(regroup_e, step - LAG_REGROUP_E, UNITS)
             at(normalise, step - LAG_NORMALISE, UNITS)
             at_block(regroup_m, step - LAG_REGROUP_M)
@@ -374,5 +419,6 @@ def tile_lorentzmultiheadattention_pb_t_kernel(
             at_block(finish, step - LAG_FINISH)
             at(transpose_e, step - LAG_TRANSPOSE_E, UNITS)
             at_block(transpose_m, step - LAG_TRANSPOSE_M)
+            at(score_on_tensor, step - LAG_SCORE_ON_TENSOR, UNITS)
             at(attend, step - LAG_ATTEND, UNITS)
             at_block(project, step - LAG_PROJECT)

@@ -1,4 +1,5 @@
 from contextlib import ExitStack
+from itertools import accumulate
 
 import concourse.masks as masks
 import concourse.mybir as mybir
@@ -16,38 +17,57 @@ PACK = 4
 BATCH, HEADS, SEQ, HEAD_DIM, OUT_DIM = 8, 2, 512, 256, 256
 MODEL_DIM = HEADS * HEAD_DIM
 ROW_TILES = SEQ // P
-PAIR = 2
-BLOCKS_PER_BATCH = ROW_TILES // PAIR
-GROUP_TILES = 2 * ROW_TILES
-BLOCKS = BATCH * BLOCKS_PER_BATCH
-UNITS = BLOCKS * HEADS
 ALL_HEADS = BATCH * HEADS
-SCALAR_HEADS = 8
+GROUP_TILES = 2 * ROW_TILES
 INV_SCALE = 1.0 / 16.0
-TENSOR_SCORED = range(7, UNITS, 8)
 
-LAG_SCORE_ON_TENSOR = -2
-LAG_SCORE = -1
-LAG_EXP = 0
-LAG_TRANSPOSE_E = 1
-LAG_REGROUP_E = 2
-LAG_QUANTISE_E = 3
-LAG_ATTEND = 4
-LAG_NORMALISE = 5
-LAG_TRANSPOSE_M = 7
-LAG_REGROUP_M = 8
-LAG_QUANTISE_M = 9
-LAG_PROJECT = 10
-LAG_BIAS = 11
-LAG_SQUARES = 12
-LAG_FINISH = 13
+BLOCK_SIZES = {0: (1, 1, 2), BATCH - 1: (2, 1, 1)}
+BLOCKS = [
+    (b, sum(sizes[:i]), sizes[i])
+    for b in range(BATCH)
+    for sizes in [BLOCK_SIZES.get(b, (2, 2))]
+    for i in range(len(sizes))
+]
+UNITS = [(c, h) for c in range(len(BLOCKS)) for h in range(HEADS)]
+UNIT_END = list(accumulate(BLOCKS[c][2] / 2 for c, h in UNITS))
+BLOCK_END = UNIT_END[HEADS - 1 :: HEADS]
+
+PAIRED = range(2, len(BLOCKS))
+TENSOR_SCORED = (0, 1, 8, 18, 28, 34)
+SCALAR_HEADS = 4
+VECTOR_SQUARES = 10
+
+SCORE_ON_TENSOR = -2.0
+SCORE = -1.0
+MAXIMUM = -0.75
+SHIFT = -0.25
+EXP = 1.0
+TRANSPOSE_E = 1.75
+REGROUP_E = 2.25
+QUANTISE_E = 3.75
+INVERT = 4.75
+ATTEND = 5.75
+NORMALISE = 6.25
+TRANSPOSE_M = 6.5
+REGROUP_M = 7.25
+QUANTISE_M = 8.25
+PROJECT = 8.5
+BIAS = 9.25
+SQUARES = 10.0
+FINISH = 10.75
+VALUES_ON_VECTOR = -1.75
+VALUES_ON_SCALAR = -2.5
+FIRST_VALUES = 2.0
+QUANTISE_VALUES = 2.25
+WO_TIMES = (1.0, 2.5, 3.5)
 
 FLOPS = 2 * BATCH * HEADS * SEQ * SEQ * HEAD_DIM + 2 * BATCH * SEQ * MODEL_DIM * OUT_DIM
 
 
 def transpose_rows(nc, psum, tag, bufs, identity, rows):
-    bank = psum.tile([P, PAIR, 2, P], F32, tag=tag, bufs=bufs)
-    for a in range(PAIR):
+    tiles = rows.shape[1]
+    bank = psum.tile([P, tiles, 2, P], F32, tag=tag, bufs=bufs)
+    for a in range(tiles):
         words = rows[:, a, :].bitcast(F32)
         for u in range(2):
             nc.tensor.transpose(
@@ -56,10 +76,8 @@ def transpose_rows(nc, psum, tag, bufs, identity, rows):
     return bank
 
 
-def regroup(nc, pool, bank, name):
-    grouped = pool.tile([P, PAIR, P, PACK], BF16, align_bytes=64, name=name)
-    nc.scalar.copy(out=grouped[:].bitcast(F32), in_=bank[:].rearrange("p a u r -> p a r u"))
-    return grouped
+def regroup(nc, grouped, bank):
+    nc.scalar.copy(out=grouped.bitcast(F32), in_=bank[:].rearrange("p a u r -> p a r u"))
 
 
 def quantise(nc, pool, grouped, name):
@@ -70,16 +88,17 @@ def quantise(nc, pool, grouped, name):
     return codes, scales
 
 
-def multiply(nc, product, rows, tile_index, columns):
+def multiply(nc, product, rows, row_tile, columns, first_column):
     row_codes, row_scales = rows
     column_codes, column_scales = columns
-    tile_columns = slice(tile_index * P, (tile_index + 1) * P)
+    stationary = slice(row_tile * P, (row_tile + 1) * P)
+    moving = slice(first_column, first_column + OUT_DIM)
     nc.tensor.matmul_mx(
         out=product,
-        lhsT=row_codes[:, tile_columns].bitcast(FP8X4),
-        lhsT_scale=row_scales[:, tile_columns],
-        rhs=column_codes[:].bitcast(FP8X4),
-        rhs_scale=column_scales[:],
+        lhsT=row_codes[:, stationary].bitcast(FP8X4),
+        lhsT_scale=row_scales[:, stationary],
+        rhs=column_codes[:, moving].bitcast(FP8X4),
+        rhs_scale=column_scales[:, moving],
         start=True,
         stop=True,
     )
@@ -93,259 +112,327 @@ def tile_lorentzmultiheadattention_pb_t_kernel(
         ctx.enter_context(tc.manual_schedule())
         const = ctx.enter_context(tc.tile_pool(name="const", bufs=1))
         inputs = ctx.enter_context(tc.tile_pool(name="inputs", bufs=ALL_HEADS))
-        work = ctx.enter_context(tc.tile_pool(name="work", bufs=3))
-        kept = ctx.enter_context(tc.tile_pool(name="kept", bufs=5))
-        groups = ctx.enter_context(tc.tile_pool(name="groups", bufs=2))
+        by_batch = ctx.enter_context(tc.tile_pool(name="by_batch", bufs=BATCH))
+        work = ctx.enter_context(tc.tile_pool(name="work", bufs=4))
+        kept = ctx.enter_context(tc.tile_pool(name="kept", bufs=10))
+        groups = ctx.enter_context(tc.tile_pool(name="groups", bufs=3))
+        values = ctx.enter_context(tc.tile_pool(name="values", bufs=4))
         psum = ctx.enter_context(tc.psum_pool(name="psum", bufs=2))
 
-        def place(u):
-            c, h = u // HEADS, u % HEADS
-            b, pair = c // BLOCKS_PER_BATCH, c % BLOCKS_PER_BATCH
-            return b * HEADS + h, pair * PAIR
-
         tq_rows = const.tile([P, SEQ], BF16)
-        nc.vector.memset(tq_rows[:], 0.0)
+        nc.vector.memset(tq_rows[:].bitcast(U32), 0)
+        tk_row_of = {}
+
+        def make_tk_row(u):
+            tk_row = const.tile([P, SEQ], BF16, name="tk_row_" + str(u))
+            nc.vector.memset(tk_row[:].bitcast(U32), 0)
+            tk_row_of[u] = tk_row
+
+        for u in TENSOR_SCORED[:HEADS]:
+            make_tk_row(u)
         identity_bf16 = const.tile([P, P], BF16)
         masks.make_identity(nc, identity_bf16[:])
         identity = const.tile([P, P], F32)
         masks.make_identity(nc, identity[:])
         minus_identity = const.tile([P, P], BF16)
         nc.vector.tensor_scalar_mul(out=minus_identity[:], in0=identity_bf16[:], scalar1=-1.0)
+        for u in TENSOR_SCORED[HEADS:]:
+            make_tk_row(u)
         half = const.tile([P, GROUP_TILES], F32)
         nc.gpsimd.memset(half[:], 0.5)
 
-        qk_tiles, v_tiles, tk_tiles = [], [], []
+        qk_tiles, v_tiles, tk_tiles = {}, {}, {}
         wo_rows = const.tile([P, 2, MODEL_DIM], BF16)
         bias = const.tile([P, OUT_DIM], BF16)
 
         def load_tk(b):
-            tk_all = inputs.tile([P, HEADS, SEQ], BF16)
+            tk_all = by_batch.tile([P, HEADS, SEQ], BF16)
             nc.sync.dma_start(out=tk_all[:], in_=tk[b].partition_broadcast(P))
-            tk_tiles.append(tk_all)
+            tk_tiles[b] = tk_all
 
-        def load_qk(n):
-            qk_rows = inputs.tile([P, ROW_TILES, SEQ], BF16)
-            qk_tiles.append(qk_rows)
-            return qk_space[n // HEADS, n % HEADS].rearrange("(p t) j -> p t j", t=ROW_TILES)
+        def load_tk_row(u):
+            c, h = UNITS[u]
+            b = BLOCKS[c][0]
+            n = b * HEADS + h
+            nc.sync.dma_start(out=tk_row_of[u][n : n + 1, :], in_=tk[b, h : h + 1])
 
-        def load_v(n):
+        def load_qk(b, h, first, tiles):
+            if first == 0:
+                qk_rows = inputs.tile([P, ROW_TILES, SEQ], BF16)
+                qk_tiles[b, h] = qk_rows
+            rows = qk_space[b, h].rearrange("(p t) j -> p t j", t=ROW_TILES)
+            span = slice(first, first + tiles)
+            nc.sync.dma_start(out=qk_tiles[b, h][:, span, :], in_=rows[:, span, :])
+
+        def load_v(b, h):
             v_rows = inputs.tile([P, PACK, HEAD_DIM], BF16)
             nc.sync.dma_start(
-                out=v_rows[:],
-                in_=v_space[n // HEADS, n % HEADS].rearrange("(p t) d -> p t d", t=PACK),
+                out=v_rows[:], in_=v_space[b, h].rearrange("(p t) d -> p t d", t=PACK)
             )
-            v_tiles.append(v_rows)
+            v_tiles[b, h] = v_rows
 
-        load_tk(0)
-        first_qk = [load_qk(h) for h in range(HEADS)]
-        for pair in range(BLOCKS_PER_BATCH):
-            tiles = slice(pair * PAIR, (pair + 1) * PAIR)
-            for h in range(HEADS):
-                nc.sync.dma_start(out=qk_tiles[h][:, tiles, :], in_=first_qk[h][:, tiles, :])
-                if pair == 0 and h == 0:
-                    nc.sync.dma_start(
-                        out=tq_rows[0:ALL_HEADS, :], in_=tq.rearrange("b h i -> (b h) i")
-                    )
-            if pair == 0:
-                nc.sync.dma_start(out=wo_rows[:], in_=Wo.rearrange("(a p) k -> p a k", p=P))
+        nc.sync.dma_start(out=tq_rows[0:ALL_HEADS, :], in_=tq.rearrange("b h i -> (b h) i"))
+        for u in TENSOR_SCORED[:HEADS]:
+            load_tk_row(u)
+        for c, (b, first, tiles) in enumerate(BLOCKS):
+            if b == 0:
                 for h in range(HEADS):
-                    load_v(h)
+                    load_qk(b, h, first, tiles)
+                if c == 0:
+                    load_tk(0)
+                if c == 1:
+                    nc.sync.dma_start(out=wo_rows[:], in_=Wo.rearrange("(a p) k -> p a k", p=P))
+                    for h in range(HEADS):
+                        load_v(0, h)
         nc.sync.dma_start(out=bias[:], in_=bo.partition_broadcast(P))
-        tk_row_of = {}
-        for u in TENSOR_SCORED:
-            n = place(u)[0]
-            tk_row = const.tile([P, SEQ], BF16, name="tk_row_" + str(u))
-            nc.vector.memset(tk_row[:], 0.0)
-            nc.sync.dma_start(
-                out=tk_row[n : n + 1, :], in_=tk[n // HEADS, n % HEADS : n % HEADS + 1]
-            )
-            tk_row_of[u] = tk_row
+        for u in TENSOR_SCORED[HEADS:]:
+            load_tk_row(u)
         for b in range(1, BATCH):
             load_tk(b)
             for h in range(HEADS):
-                n = b * HEADS + h
-                qk_rows_hbm = load_qk(n)
-                nc.sync.dma_start(out=qk_tiles[n][:], in_=qk_rows_hbm)
+                load_qk(b, h, 0, ROW_TILES)
             for h in range(HEADS):
-                load_v(b * HEADS + h)
+                load_v(b, h)
 
-        tq_bank = psum.tile([P, ROW_TILES, P], BF16, tag="y", bufs=1)
-        for t in range(ROW_TILES):
-            nc.tensor.transpose(
-                out=tq_bank[:, t, :], in_=tq_rows[:, t:SEQ:ROW_TILES], identity=identity_bf16[:]
-            )
         tq_columns = const.tile([P, ROW_TILES, ALL_HEADS], F32)
-        nc.vector.tensor_copy(out=tq_columns[:], in_=tq_bank[:, :, 0:ALL_HEADS])
 
-        v_grouped_of, v_mx_of = {}, {}
+        def prepare_tq(u):
+            tq_bank = psum.tile([P, ROW_TILES, P], BF16, tag="y", bufs=1)
+            for t in range(ROW_TILES):
+                nc.tensor.transpose(
+                    out=tq_bank[:, t, :],
+                    in_=tq_rows[:, t:SEQ:ROW_TILES],
+                    identity=identity_bf16[:],
+                )
+            nc.vector.tensor_copy(out=tq_columns[:], in_=tq_bank[:, :, 0:ALL_HEADS])
+
+        v_grouped_of, v_mx_of, wo_of = {}, {}, {}
         scores_of, top_of, shift_of, e_rows_of, rowsum_of = {}, {}, {}, {}, {}
         e_bank_of, e_grouped_of, e_mx_of, inv_rowsum_of, z_of = {}, {}, {}, {}, {}
         merged_of, m_bank_of, m_grouped_of, m_mx_of = {}, {}, {}, {}
         y_of, result_of, norm_of = {}, {}, {}
 
-        def group_place(c):
-            return divmod(c * PAIR, GROUP_TILES)
+        def shared(u):
+            c, h = UNITS[u]
+            if c in PAIRED:
+                return c * HEADS, h, HEADS
+            return u, 0, 1
+
+        def rows_of_out(c):
+            b, first, tiles = BLOCKS[c]
+            group, place = divmod(b * ROW_TILES + first, GROUP_TILES)
+            return group, range(place, place + tiles)
 
         def score_products(u):
             if u in TENSOR_SCORED:
                 return
-            n, first = place(u)
-            scores = work.tile([P, PAIR, SEQ], F32)
-            for a in range(PAIR):
+            c, h = UNITS[u]
+            b, first, tiles = BLOCKS[c]
+            scores = work.tile([P, tiles, SEQ], F32, bufs=4)
+            for a in range(tiles):
                 nc.vector.scalar_tensor_tensor(
                     out=scores[:, a, :],
-                    in0=tk_tiles[n // HEADS][:, n % HEADS, :],
-                    scalar=tq_columns[:, first + a, n : n + 1],
-                    in1=qk_tiles[n][:, first + a, :],
+                    in0=tk_tiles[b][:, h, :],
+                    scalar=tq_columns[:, first + a, b * HEADS + h : b * HEADS + h + 1],
+                    in1=qk_tiles[b, h][:, first + a, :],
                     op0=ALU.mult,
                     op1=ALU.subtract,
                 )
-            scores_of[u] = [scores[:, a, :] for a in range(PAIR)]
+            scores_of[u] = [scores[:, a, :] for a in range(tiles)]
 
         def score_maxima(u):
-            top = work.tile([P, PAIR], F32)
-            for a in range(PAIR):
+            key, i, count = shared(u)
+            tiles = BLOCKS[UNITS[u][0]][2]
+            if i == 0:
+                top = kept.tile([P, count, tiles], F32)
+                top_of[key] = top
+            for a in range(tiles):
                 nc.vector.tensor_reduce(
-                    out=top[:, a : a + 1],
+                    out=top_of[key][:, i, a : a + 1],
                     in_=scores_of[u][a],
                     axis=mybir.AxisListType.X,
                     op=ALU.max,
                 )
-            top_of[u] = top
 
         def score_shift(u):
-            shift = work.tile([P, PAIR], F32)
-            nc.vector.tensor_scalar_mul(out=shift[:], in0=top_of[u][:], scalar1=-INV_SCALE)
-            shift_of[u] = shift
+            key, i, count = shared(u)
+            if i + 1 < count:
+                return
+            shift = kept.tile([P, count, BLOCKS[UNITS[u][0]][2]], F32)
+            nc.vector.tensor_scalar_mul(out=shift[:], in0=top_of[key][:], scalar1=-INV_SCALE)
+            shift_of[key] = shift
 
         def regroup_values(n):
-            v_grouped = work.tile([P, HEAD_DIM, PACK], BF16, align_bytes=64)
-            copy = nc.scalar.copy if n < SCALAR_HEADS else nc.vector.tensor_copy
+            b, h = divmod(n, HEADS)
+            if h == 0:
+                v_grouped = work.tile([P, HEADS, HEAD_DIM, PACK], BF16, align_bytes=64, bufs=2)
+                v_grouped_of[b] = v_grouped
+            copy = nc.scalar.copy if v_on_scalar(n) else nc.vector.tensor_copy
             copy(
-                out=v_grouped[:].rearrange("p (c i) t -> p c t i", i=4),
-                in_=v_tiles[n][:].rearrange("p t (c i) -> p c t i", i=4),
+                out=v_grouped_of[b][:, h].rearrange("p (c i) t -> p c t i", i=4),
+                in_=v_tiles[b, h][:].rearrange("p t (c i) -> p c t i", i=4),
             )
-            v_grouped_of[n] = v_grouped
 
-        def quantise_values(n):
-            v_mx_of[n] = quantise(nc, inputs, v_grouped_of[n][:].rearrange("p d t -> p (d t)"), "v")
+        def quantise_values(b):
+            v_mx_of[b] = quantise(
+                nc, values, v_grouped_of[b][:].rearrange("p h d t -> p (h d t)"), "v"
+            )
 
         def quantise_e(u):
-            e_mx_of[u] = quantise(
-                nc, work, e_grouped_of[u][:].rearrange("p a r t -> p (a r t)"), "e"
+            key, i, count = shared(u)
+            if i + 1 < count:
+                return
+            e_mx_of[key] = quantise(
+                nc, work, e_grouped_of[key][:].rearrange("p i a r t -> p (i a r t)"), "e"
             )
 
         def invert_rowsum(u):
-            inv_rowsum = kept.tile([P, PAIR], F32)
-            nc.vector.reciprocal(out=inv_rowsum[:], in_=rowsum_of[u][:])
-            inv_rowsum_of[u] = inv_rowsum
+            key, i, count = shared(u)
+            if i + 1 < count:
+                return
+            inv_rowsum = kept.tile([P, count, BLOCKS[UNITS[u][0]][2]], F32)
+            nc.vector.reciprocal(out=inv_rowsum[:], in_=rowsum_of[key][:])
+            inv_rowsum_of[key] = inv_rowsum
 
         def quantise_m(c):
             m_mx_of[c] = quantise(
                 nc, work, m_grouped_of[c][:].rearrange("p a r t -> p (a r t)"), "m"
             )
 
+        def quantise_wo(u):
+            wo_of["mx"] = quantise(
+                nc, const, wo_of["grouped"][:].rearrange("p a r t -> p (a r t)"), "wo"
+            )
+
         def add_bias(c):
-            group, first = group_place(c)
-            if first == 0:
+            group, place = rows_of_out(c)
+            if place[0] == 0:
                 result = groups.tile([P, GROUP_TILES, 1 + OUT_DIM], F32)
                 norm = groups.tile([P, GROUP_TILES], F32)
                 result_of[group], norm_of[group] = result, norm
             nc.vector.tensor_tensor(
-                out=result_of[group][:, first : first + PAIR, 1:],
+                out=result_of[group][:, place[0] : place[-1] + 1, 1:],
                 in0=y_of[c][:],
-                in1=bias[:].unsqueeze(1).to_broadcast([P, PAIR, OUT_DIM]),
+                in1=bias[:].unsqueeze(1).to_broadcast([P, len(place), OUT_DIM]),
                 op=ALU.add,
             )
 
         def finish(c):
-            group, first = group_place(c)
-            if c < BLOCKS - GROUP_TILES // PAIR:
-                if first + PAIR < GROUP_TILES:
-                    return
-                tiles = range(0, GROUP_TILES)
+            group, place = rows_of_out(c)
+            last_group = (group + 1) * GROUP_TILES == BATCH * ROW_TILES
+            if last_group:
+                span = slice(place[0], place[-1] + 1)
+                nc.scalar.activation(
+                    out=result_of[group][:, span, 0],
+                    in_=norm_of[group][:, span],
+                    func=ACT.Sqrt,
+                    bias=1.0,
+                )
+                stores = [place]
             else:
-                tiles = range(first, first + PAIR)
-            span = slice(tiles[0], tiles[-1] + 1)
-            radicand = groups.tile([P, GROUP_TILES], F32)
-            nc.gpsimd.tensor_scalar(
-                out=radicand[:, span],
-                in0=norm_of[group][:, span],
-                scalar1=1.0,
-                scalar2=None,
-                op0=ALU.add,
-            )
-            nc.gpsimd.tensor_tensor(
-                out=result_of[group][:, span, 0],
-                in0=radicand[:, span],
-                in1=half[:, span],
-                op=ALU.pow,
-            )
-            store_tiles = min(len(tiles), ROW_TILES)
-            for start in range(tiles[0], tiles[-1] + 1, store_tiles):
-                b = group * (GROUP_TILES // ROW_TILES) + start // ROW_TILES
-                t = start % ROW_TILES
+                if place[-1] + 1 < GROUP_TILES:
+                    return
+                radicand = groups.tile([P, GROUP_TILES], F32)
+                nc.gpsimd.tensor_scalar(
+                    out=radicand[:],
+                    in0=norm_of[group][:],
+                    scalar1=1.0,
+                    scalar2=None,
+                    op0=ALU.add,
+                )
+                nc.gpsimd.tensor_tensor(
+                    out=result_of[group][:, :, 0], in0=radicand[:], in1=half[:], op=ALU.pow
+                )
+                stores = [range(t, t + ROW_TILES) for t in range(0, GROUP_TILES, ROW_TILES)]
+            for tiles in stores:
+                b, t = divmod(group * GROUP_TILES + tiles[0], ROW_TILES)
                 rows = out[b].rearrange("(p t) o -> p t o", t=ROW_TILES)
                 nc.sync.dma_start(
-                    out=rows[:, t : t + store_tiles, :],
-                    in_=result_of[group][:, start : start + store_tiles, :],
+                    out=rows[:, t : t + len(tiles), :],
+                    in_=result_of[group][:, tiles[0] : tiles[-1] + 1, :],
                 )
 
         def exponentiate(u):
-            e_rows = work.tile([P, PAIR, SEQ], BF16)
-            rowsum = kept.tile([P, PAIR], F32)
-            for a in range(PAIR):
+            key, i, count = shared(u)
+            tiles = BLOCKS[UNITS[u][0]][2]
+            e_rows = work.tile([P, tiles, SEQ], BF16, bufs=4)
+            if i == 0:
+                rowsum = kept.tile([P, count, tiles], F32)
+                rowsum_of[key] = rowsum
+            for a in range(tiles):
                 nc.scalar.activation(
                     out=e_rows[:, a, :],
                     in_=scores_of[u][a],
                     func=ACT.Exp,
-                    bias=shift_of[u][:, a : a + 1],
+                    bias=shift_of[key][:, i, a : a + 1],
                     scale=INV_SCALE,
-                    accum_out=rowsum[:, a : a + 1],
+                    accum_out=rowsum_of[key][:, i, a : a + 1],
                 )
-            e_rows_of[u], rowsum_of[u] = e_rows, rowsum
+            e_rows_of[u] = e_rows
 
         def regroup_e(u):
-            e_grouped_of[u] = regroup(nc, work, e_bank_of[u], "e_grouped")
+            key, i, count = shared(u)
+            tiles = BLOCKS[UNITS[u][0]][2]
+            if i == 0:
+                e_grouped = work.tile([P, count, tiles, P, PACK], BF16, align_bytes=64, bufs=3)
+                e_grouped_of[key] = e_grouped
+            regroup(nc, e_grouped_of[key][:, i], e_bank_of[u])
 
         def normalise(u):
-            c, h = u // HEADS, u % HEADS
+            key, i, count = shared(u)
+            c, h = UNITS[u]
+            tiles = BLOCKS[c][2]
             if h == 0:
-                merged = work.tile([P, PAIR, MODEL_DIM], BF16)
+                merged = work.tile([P, tiles, MODEL_DIM], BF16, bufs=3)
                 merged_of[c] = merged
-            for a in range(PAIR):
-                nc.scalar.activation(
-                    out=merged_of[c][:, a, h * HEAD_DIM : (h + 1) * HEAD_DIM],
-                    in_=z_of[u][:, a, :],
-                    func=ACT.Copy,
-                    scale=inv_rowsum_of[u][:, a : a + 1],
-                )
+            for a in range(tiles):
+                z_rows = merged_of[c][:, a, h * HEAD_DIM : (h + 1) * HEAD_DIM]
+                factor = inv_rowsum_of[key][:, i, a : a + 1]
+                nc.scalar.activation(out=z_rows, in_=z_of[u][:, a, :], func=ACT.Copy, scale=factor)
 
         def regroup_m(c):
-            m_grouped_of[c] = regroup(nc, work, m_bank_of[c], "m_grouped")
+            m_grouped = work.tile([P, BLOCKS[c][2], P, PACK], BF16, align_bytes=64, bufs=3)
+            regroup(nc, m_grouped[:], m_bank_of[c])
+            m_grouped_of[c] = m_grouped
+
+        def regroup_wo(u):
+            wo_grouped = const.tile([P, 2, P, PACK], BF16, align_bytes=64)
+            regroup(nc, wo_grouped[:], wo_of["bank"])
+            wo_of["grouped"] = wo_grouped
 
         def sum_squares(c):
-            group, first = group_place(c)
-            squares = work.tile([P, OUT_DIM], F32)
-            for t in range(first, first + PAIR):
-                nc.scalar.activation(
-                    out=squares[:],
-                    in_=result_of[group][:, t, 1:],
-                    func=ACT.Square,
-                    accum_out=norm_of[group][:, t : t + 1],
-                )
+            group, place = rows_of_out(c)
+            squares = work.tile([P, OUT_DIM], F32, bufs=2)
+            for t in place:
+                y_rows = result_of[group][:, t, 1:]
+                total = norm_of[group][:, t : t + 1]
+                if c >= VECTOR_SQUARES:
+                    nc.vector.scalar_tensor_tensor(
+                        out=squares[:],
+                        in0=y_rows,
+                        scalar=1.0,
+                        in1=y_rows,
+                        op0=ALU.mult,
+                        op1=ALU.mult,
+                        accum_out=total,
+                    )
+                else:
+                    nc.scalar.activation(
+                        out=squares[:], in_=y_rows, func=ACT.Square, accum_out=total
+                    )
 
         def score_on_tensor(u):
             if u not in TENSOR_SCORED:
                 return
-            n, first = place(u)
+            c, h = UNITS[u]
+            b, first, tiles = BLOCKS[c]
             scores_of[u] = []
-            for t in range(first, first + PAIR):
+            for t in range(first, first + tiles):
                 scores_bank = psum.tile([P, SEQ], F32, tag="scores", bufs=2)
                 nc.tensor.matmul(
                     out=scores_bank[:],
                     lhsT=minus_identity[:],
-                    rhs=qk_tiles[n][:, t, :],
+                    rhs=qk_tiles[b, h][:, t, :],
                     start=True,
                     stop=False,
                 )
@@ -361,64 +448,68 @@ def tile_lorentzmultiheadattention_pb_t_kernel(
         def transpose_e(u):
             e_bank_of[u] = transpose_rows(nc, psum, "e_bank", 2, identity[:], e_rows_of[u][:])
 
+        def transpose_wo(u):
+            wo_of["bank"] = transpose_rows(nc, psum, "e_bank", 2, identity[:], wo_rows[:])
+
         def attend(u):
-            n, first = place(u)
-            z_bank = psum.tile([P, PAIR, HEAD_DIM], F32, tag="z")
-            for a in range(PAIR):
-                multiply(nc, z_bank[:, a, :], e_mx_of[u], a, v_mx_of[n])
+            key, i, count = shared(u)
+            c, h = UNITS[u]
+            tiles = BLOCKS[c][2]
+            z_bank = psum.tile([P, tiles, HEAD_DIM], F32, tag="z")
+            for a in range(tiles):
+                multiply(
+                    nc, z_bank[:, a, :], e_mx_of[key], i * tiles + a, v_mx_of[BLOCKS[c][0]], h * HEAD_DIM
+                )
             z_of[u] = z_bank
 
         def transpose_m(c):
-            m_bank_of[c] = transpose_rows(
-                nc, psum, "m_bank", 1, identity[:], merged_of[c][:]
-            )
+            m_bank_of[c] = transpose_rows(nc, psum, "m_bank", 1, identity[:], merged_of[c][:])
 
         def project(c):
-            y_bank = psum.tile([P, PAIR, OUT_DIM], F32, tag="y", bufs=1)
-            for a in range(PAIR):
-                multiply(nc, y_bank[:, a, :], m_mx_of[c], a, wo_mx)
+            y_bank = psum.tile([P, BLOCKS[c][2], OUT_DIM], F32, tag="y", bufs=1)
+            for a in range(BLOCKS[c][2]):
+                multiply(nc, y_bank[:, a, :], m_mx_of[c], a, wo_of["mx"], 0)
             y_of[c] = y_bank
 
-        def at(stage, index, count):
-            if 0 <= index < count:
-                stage(index)
+        def v_on_scalar(n):
+            return n < SCALAR_HEADS or n % HEADS == 0
 
-        def at_block(stage, index):
-            if index % HEADS == 0:
-                at(stage, index // HEADS, BLOCKS)
-
-        wo_grouped = regroup(
-            nc, const, transpose_rows(nc, psum, "e_bank", 2, identity[:], wo_rows[:]), "wo_grouped"
-        )
-
-        score_products(0)
-        score_maxima(0)
-        score_shift(0)
-        wo_mx = quantise(nc, const, wo_grouped[:].rearrange("p a r t -> p (a r t)"), "wo")
-
-        for step in range(UNITS + LAG_FINISH):
-            at_block(add_bias, step - LAG_BIAS)
-            at(score_products, step - LAG_SCORE, UNITS)
-            at(score_maxima, step - LAG_SCORE, UNITS)
-            at(quantise_e, step - LAG_QUANTISE_E, UNITS)
-            at(score_shift, step - LAG_SCORE, UNITS)
-            at(invert_rowsum, step - LAG_QUANTISE_E, UNITS)
-            at_block(quantise_m, step - LAG_QUANTISE_M)
-            at(quantise_values, step - 1, SCALAR_HEADS)
-            if step // 2 >= SCALAR_HEADS:
-                if step % 2 == 0:
-                    at(regroup_values, step // 2, ALL_HEADS)
-                else:
-                    at(quantise_values, step // 2, ALL_HEADS)
-            at(exponentiate, step - LAG_EXP, UNITS)
-            at(regroup_values, step, SCALAR_HEADS)
-            at(regroup_e, step - LAG_REGROUP_E, UNITS)
-            at(normalise, step - LAG_NORMALISE, UNITS)
-            at_block(regroup_m, step - LAG_REGROUP_M)
-            at_block(sum_squares, step - LAG_SQUARES)
-            at_block(finish, step - LAG_FINISH)
-            at(transpose_e, step - LAG_TRANSPOSE_E, UNITS)
-            at_block(transpose_m, step - LAG_TRANSPOSE_M)
-            at(score_on_tensor, step - LAG_SCORE_ON_TENSOR, UNITS)
-            at(attend, step - LAG_ATTEND, UNITS)
-            at_block(project, step - LAG_PROJECT)
+        events = [(-1.6, prepare_tq, 0), (WO_TIMES[0], transpose_wo, 0), (WO_TIMES[1], regroup_wo, 0), (WO_TIMES[2], quantise_wo, 0)]
+        for stage, lag in [
+            (score_on_tensor, SCORE_ON_TENSOR),
+            (score_products, SCORE),
+            (score_maxima, MAXIMUM),
+            (score_shift, SHIFT),
+            (exponentiate, EXP),
+            (transpose_e, TRANSPOSE_E),
+            (regroup_e, REGROUP_E),
+            (quantise_e, QUANTISE_E),
+            (invert_rowsum, INVERT),
+            (attend, ATTEND),
+            (normalise, NORMALISE),
+        ]:
+            events.extend((UNIT_END[u] + lag, stage, u) for u in range(len(UNITS)))
+        for stage, lag in [
+            (transpose_m, TRANSPOSE_M),
+            (regroup_m, REGROUP_M),
+            (quantise_m, QUANTISE_M),
+            (project, PROJECT),
+            (add_bias, BIAS),
+            (sum_squares, SQUARES),
+            (finish, FINISH),
+        ]:
+            events.extend((BLOCK_END[c] + lag, stage, c) for c in range(len(BLOCKS)))
+        rooted = UNIT_END[-1] + NORMALISE + 0.05
+        events = [
+            (max(time, rooted), stage, c)
+            if stage == finish and rows_of_out(c)[0] == BATCH * ROW_TILES // GROUP_TILES - 1
+            else (time, stage, c)
+            for time, stage, c in events
+        ]
+        for n in range(ALL_HEADS):
+            t = max(FIRST_VALUES + n, HEADS * n + VALUES_ON_SCALAR) if v_on_scalar(n) else HEADS * n + VALUES_ON_VECTOR
+            events.append((t, regroup_values, n))
+            if n % 2:
+                events.append((t + QUANTISE_VALUES, quantise_values, n // 2))
+        for event in sorted(reversed(events), key=lambda event: event[0]):
+            event[1](event[2])

@@ -1,5 +1,4 @@
 from contextlib import ExitStack
-from itertools import accumulate
 
 import concourse.masks as masks
 import concourse.mybir as mybir
@@ -28,38 +27,8 @@ BLOCKS = [
     for sizes in [BLOCK_SIZES.get(b, (2, 2))]
     for i in range(len(sizes))
 ]
-UNITS = [(c, h) for c in range(len(BLOCKS)) for h in range(HEADS)]
-UNIT_END = list(accumulate(BLOCKS[c][2] / 2 for c, h in UNITS))
-BLOCK_END = UNIT_END[HEADS - 1 :: HEADS]
-
-PAIRED = range(2, len(BLOCKS))
-TENSOR_SCORED = (0, 1, 8, 18, 28, 34)
-SCALAR_HEADS = 4
-VECTOR_SQUARES = 10
-
-SCORE_ON_TENSOR = -2.0
-SCORE = -1.0
-MAXIMUM = -0.75
-SHIFT = -0.25
-EXP = 1.0
-TRANSPOSE_E = 1.75
-REGROUP_E = 2.25
-QUANTISE_E = 3.75
-INVERT = 4.75
-ATTEND = 5.75
-NORMALISE = 6.25
-TRANSPOSE_M = 6.5
-REGROUP_M = 7.25
-QUANTISE_M = 8.25
-PROJECT = 8.5
-BIAS = 9.25
-SQUARES = 10.0
-FINISH = 10.75
-VALUES_ON_VECTOR = -1.75
-VALUES_ON_SCALAR = -2.5
-FIRST_VALUES = 2.0
-QUANTISE_VALUES = 2.25
-WO_TIMES = (1.0, 2.5, 3.5)
+TENSOR_SCORED = ((1, 0), (1, 1), (4, 0), (8, 0), (12, 0), (17, 0))
+VECTOR_SQUARES = 8
 
 FLOPS = 2 * BATCH * HEADS * SEQ * SEQ * HEAD_DIM + 2 * BATCH * SEQ * MODEL_DIM * OUT_DIM
 
@@ -116,28 +85,26 @@ def tile_lorentzmultiheadattention_pb_t_kernel(
         work = ctx.enter_context(tc.tile_pool(name="work", bufs=4))
         kept = ctx.enter_context(tc.tile_pool(name="kept", bufs=10))
         groups = ctx.enter_context(tc.tile_pool(name="groups", bufs=3))
-        values = ctx.enter_context(tc.tile_pool(name="values", bufs=4))
+        values = ctx.enter_context(tc.tile_pool(name="values", bufs=3))
         psum = ctx.enter_context(tc.psum_pool(name="psum", bufs=2))
 
         tq_rows = const.tile([P, SEQ], BF16)
         nc.vector.memset(tq_rows[:].bitcast(U32), 0)
         tk_row_of = {}
 
-        def make_tk_row(u):
-            tk_row = const.tile([P, SEQ], BF16, name="tk_row_" + str(u))
+        def make_tk_row(c, h):
+            tk_row = const.tile([P, SEQ], BF16, name="tk_row_%d_%d" % (c, h))
             nc.vector.memset(tk_row[:].bitcast(U32), 0)
-            tk_row_of[u] = tk_row
+            tk_row_of[c, h] = tk_row
 
-        for u in TENSOR_SCORED[:HEADS]:
-            make_tk_row(u)
         identity_bf16 = const.tile([P, P], BF16)
         masks.make_identity(nc, identity_bf16[:])
         identity = const.tile([P, P], F32)
         masks.make_identity(nc, identity[:])
         minus_identity = const.tile([P, P], BF16)
         nc.vector.tensor_scalar_mul(out=minus_identity[:], in0=identity_bf16[:], scalar1=-1.0)
-        for u in TENSOR_SCORED[HEADS:]:
-            make_tk_row(u)
+        for c, h in TENSOR_SCORED:
+            make_tk_row(c, h)
         half = const.tile([P, GROUP_TILES], F32)
         nc.gpsimd.memset(half[:], 0.5)
 
@@ -150,11 +117,10 @@ def tile_lorentzmultiheadattention_pb_t_kernel(
             nc.sync.dma_start(out=tk_all[:], in_=tk[b].partition_broadcast(P))
             tk_tiles[b] = tk_all
 
-        def load_tk_row(u):
-            c, h = UNITS[u]
+        def load_tk_row(c, h):
             b = BLOCKS[c][0]
             n = b * HEADS + h
-            nc.sync.dma_start(out=tk_row_of[u][n : n + 1, :], in_=tk[b, h : h + 1])
+            nc.sync.dma_start(out=tk_row_of[c, h][n : n + 1, :], in_=tk[b, h : h + 1])
 
         def load_qk(b, h, first, tiles):
             if first == 0:
@@ -172,21 +138,21 @@ def tile_lorentzmultiheadattention_pb_t_kernel(
             v_tiles[b, h] = v_rows
 
         nc.sync.dma_start(out=tq_rows[0:ALL_HEADS, :], in_=tq.rearrange("b h i -> (b h) i"))
-        for u in TENSOR_SCORED[:HEADS]:
-            load_tk_row(u)
+        load_tk(0)
         for c, (b, first, tiles) in enumerate(BLOCKS):
             if b == 0:
                 for h in range(HEADS):
                     load_qk(b, h, first, tiles)
                 if c == 0:
-                    load_tk(0)
+                    for h in range(HEADS):
+                        load_tk_row(1, h)
                 if c == 1:
                     nc.sync.dma_start(out=wo_rows[:], in_=Wo.rearrange("(a p) k -> p a k", p=P))
                     for h in range(HEADS):
                         load_v(0, h)
         nc.sync.dma_start(out=bias[:], in_=bo.partition_broadcast(P))
-        for u in TENSOR_SCORED[HEADS:]:
-            load_tk_row(u)
+        for c, h in TENSOR_SCORED[HEADS:]:
+            load_tk_row(c, h)
         for b in range(1, BATCH):
             load_tk(b)
             for h in range(HEADS):
@@ -196,15 +162,12 @@ def tile_lorentzmultiheadattention_pb_t_kernel(
 
         tq_columns = const.tile([P, ROW_TILES, ALL_HEADS], F32)
 
-        def prepare_tq(u):
-            tq_bank = psum.tile([P, ROW_TILES, P], BF16, tag="y", bufs=1)
-            for t in range(ROW_TILES):
-                nc.tensor.transpose(
-                    out=tq_bank[:, t, :],
-                    in_=tq_rows[:, t:SEQ:ROW_TILES],
-                    identity=identity_bf16[:],
-                )
-            nc.vector.tensor_copy(out=tq_columns[:], in_=tq_bank[:, :, 0:ALL_HEADS])
+        tq_bank = psum.tile([P, ROW_TILES, P], BF16, tag="y", bufs=1)
+        for t in range(ROW_TILES):
+            nc.tensor.transpose(
+                out=tq_bank[:, t, :], in_=tq_rows[:, t:SEQ:ROW_TILES], identity=identity_bf16[:]
+            )
+        nc.vector.tensor_copy(out=tq_columns[:], in_=tq_bank[:, :, 0:ALL_HEADS])
 
         v_grouped_of, v_mx_of, wo_of = {}, {}, {}
         scores_of, top_of, shift_of, e_rows_of, rowsum_of = {}, {}, {}, {}, {}
@@ -212,23 +175,16 @@ def tile_lorentzmultiheadattention_pb_t_kernel(
         merged_of, m_bank_of, m_grouped_of, m_mx_of = {}, {}, {}, {}
         y_of, result_of, norm_of = {}, {}, {}
 
-        def shared(u):
-            c, h = UNITS[u]
-            if c in PAIRED:
-                return c * HEADS, h, HEADS
-            return u, 0, 1
-
         def rows_of_out(c):
             b, first, tiles = BLOCKS[c]
             group, place = divmod(b * ROW_TILES + first, GROUP_TILES)
             return group, range(place, place + tiles)
 
-        def score_products(u):
-            if u in TENSOR_SCORED:
+        def score_products(c, h):
+            if (c, h) in TENSOR_SCORED:
                 return
-            c, h = UNITS[u]
             b, first, tiles = BLOCKS[c]
-            scores = work.tile([P, tiles, SEQ], F32, bufs=4)
+            scores = work.tile([P, tiles, SEQ], F32)
             for a in range(tiles):
                 nc.vector.scalar_tensor_tensor(
                     out=scores[:, a, :],
@@ -238,36 +194,31 @@ def tile_lorentzmultiheadattention_pb_t_kernel(
                     op0=ALU.mult,
                     op1=ALU.subtract,
                 )
-            scores_of[u] = [scores[:, a, :] for a in range(tiles)]
+            scores_of[c, h] = [scores[:, a, :] for a in range(tiles)]
 
-        def score_maxima(u):
-            key, i, count = shared(u)
-            tiles = BLOCKS[UNITS[u][0]][2]
-            if i == 0:
-                top = kept.tile([P, count, tiles], F32)
-                top_of[key] = top
+        def score_maxima(c, h):
+            tiles = BLOCKS[c][2]
+            if h == 0:
+                top = kept.tile([P, HEADS, tiles], F32)
+                top_of[c] = top
             for a in range(tiles):
                 nc.vector.tensor_reduce(
-                    out=top_of[key][:, i, a : a + 1],
-                    in_=scores_of[u][a],
+                    out=top_of[c][:, h, a : a + 1],
+                    in_=scores_of[c, h][a],
                     axis=mybir.AxisListType.X,
                     op=ALU.max,
                 )
 
-        def score_shift(u):
-            key, i, count = shared(u)
-            if i + 1 < count:
-                return
-            shift = kept.tile([P, count, BLOCKS[UNITS[u][0]][2]], F32)
-            nc.vector.tensor_scalar_mul(out=shift[:], in0=top_of[key][:], scalar1=-INV_SCALE)
-            shift_of[key] = shift
+        def score_shift(c):
+            shift = kept.tile([P, HEADS, BLOCKS[c][2]], F32)
+            nc.vector.tensor_scalar_mul(out=shift[:], in0=top_of[c][:], scalar1=-INV_SCALE)
+            shift_of[c] = shift
 
-        def regroup_values(n):
-            b, h = divmod(n, HEADS)
+        def regroup_values(b, h):
             if h == 0:
                 v_grouped = work.tile([P, HEADS, HEAD_DIM, PACK], BF16, align_bytes=64, bufs=2)
                 v_grouped_of[b] = v_grouped
-            copy = nc.scalar.copy if v_on_scalar(n) else nc.vector.tensor_copy
+            copy = nc.vector.tensor_copy if b >= 2 and h == 1 else nc.scalar.copy
             copy(
                 out=v_grouped_of[b][:, h].rearrange("p (c i) t -> p c t i", i=4),
                 in_=v_tiles[b, h][:].rearrange("p t (c i) -> p c t i", i=4),
@@ -278,28 +229,22 @@ def tile_lorentzmultiheadattention_pb_t_kernel(
                 nc, values, v_grouped_of[b][:].rearrange("p h d t -> p (h d t)"), "v"
             )
 
-        def quantise_e(u):
-            key, i, count = shared(u)
-            if i + 1 < count:
-                return
-            e_mx_of[key] = quantise(
-                nc, work, e_grouped_of[key][:].rearrange("p i a r t -> p (i a r t)"), "e"
+        def quantise_e(c):
+            e_mx_of[c] = quantise(
+                nc, work, e_grouped_of[c][:].rearrange("p h a r t -> p (h a r t)"), "e"
             )
 
-        def invert_rowsum(u):
-            key, i, count = shared(u)
-            if i + 1 < count:
-                return
-            inv_rowsum = kept.tile([P, count, BLOCKS[UNITS[u][0]][2]], F32)
-            nc.vector.reciprocal(out=inv_rowsum[:], in_=rowsum_of[key][:])
-            inv_rowsum_of[key] = inv_rowsum
+        def invert_rowsum(c):
+            inv_rowsum = kept.tile([P, HEADS, BLOCKS[c][2]], F32)
+            nc.vector.reciprocal(out=inv_rowsum[:], in_=rowsum_of[c][:])
+            inv_rowsum_of[c] = inv_rowsum
 
         def quantise_m(c):
             m_mx_of[c] = quantise(
                 nc, work, m_grouped_of[c][:].rearrange("p a r t -> p (a r t)"), "m"
             )
 
-        def quantise_wo(u):
+        def quantise_wo():
             wo_of["mx"] = quantise(
                 nc, const, wo_of["grouped"][:].rearrange("p a r t -> p (a r t)"), "wo"
             )
@@ -352,58 +297,56 @@ def tile_lorentzmultiheadattention_pb_t_kernel(
                     in_=result_of[group][:, tiles[0] : tiles[-1] + 1, :],
                 )
 
-        def exponentiate(u):
-            key, i, count = shared(u)
-            tiles = BLOCKS[UNITS[u][0]][2]
-            e_rows = work.tile([P, tiles, SEQ], BF16, bufs=4)
-            if i == 0:
-                rowsum = kept.tile([P, count, tiles], F32)
-                rowsum_of[key] = rowsum
+        def exponentiate(c, h):
+            tiles = BLOCKS[c][2]
+            e_rows = work.tile([P, tiles, SEQ], BF16)
+            if h == 0:
+                rowsum = kept.tile([P, HEADS, tiles], F32)
+                rowsum_of[c] = rowsum
             for a in range(tiles):
                 nc.scalar.activation(
                     out=e_rows[:, a, :],
-                    in_=scores_of[u][a],
+                    in_=scores_of[c, h][a],
                     func=ACT.Exp,
-                    bias=shift_of[key][:, i, a : a + 1],
+                    bias=shift_of[c][:, h, a : a + 1],
                     scale=INV_SCALE,
-                    accum_out=rowsum_of[key][:, i, a : a + 1],
+                    accum_out=rowsum_of[c][:, h, a : a + 1],
                 )
-            e_rows_of[u] = e_rows
+            e_rows_of[c, h] = e_rows
 
-        def regroup_e(u):
-            key, i, count = shared(u)
-            tiles = BLOCKS[UNITS[u][0]][2]
-            if i == 0:
-                e_grouped = work.tile([P, count, tiles, P, PACK], BF16, align_bytes=64, bufs=3)
-                e_grouped_of[key] = e_grouped
-            regroup(nc, e_grouped_of[key][:, i], e_bank_of[u])
+        def regroup_e(c, h):
+            if h == 0:
+                e_grouped = work.tile([P, HEADS, BLOCKS[c][2], P, PACK], BF16, align_bytes=64)
+                e_grouped_of[c] = e_grouped
+            regroup(nc, e_grouped_of[c][:, h], e_bank_of[c, h])
 
-        def normalise(u):
-            key, i, count = shared(u)
-            c, h = UNITS[u]
+        def normalise(c, h):
             tiles = BLOCKS[c][2]
             if h == 0:
                 merged = work.tile([P, tiles, MODEL_DIM], BF16, bufs=3)
                 merged_of[c] = merged
             for a in range(tiles):
-                z_rows = merged_of[c][:, a, h * HEAD_DIM : (h + 1) * HEAD_DIM]
-                factor = inv_rowsum_of[key][:, i, a : a + 1]
-                nc.scalar.activation(out=z_rows, in_=z_of[u][:, a, :], func=ACT.Copy, scale=factor)
+                nc.scalar.activation(
+                    out=merged_of[c][:, a, h * HEAD_DIM : (h + 1) * HEAD_DIM],
+                    in_=z_of[c, h][:, a, :],
+                    func=ACT.Copy,
+                    scale=inv_rowsum_of[c][:, h, a : a + 1],
+                )
 
         def regroup_m(c):
             m_grouped = work.tile([P, BLOCKS[c][2], P, PACK], BF16, align_bytes=64, bufs=3)
             regroup(nc, m_grouped[:], m_bank_of[c])
             m_grouped_of[c] = m_grouped
 
-        def regroup_wo(u):
+        def regroup_wo():
             wo_grouped = const.tile([P, 2, P, PACK], BF16, align_bytes=64)
             regroup(nc, wo_grouped[:], wo_of["bank"])
             wo_of["grouped"] = wo_grouped
 
         def sum_squares(c):
             group, place = rows_of_out(c)
-            squares = work.tile([P, OUT_DIM], F32, bufs=2)
             for t in place:
+                squares = work.tile([P, OUT_DIM], F32, bufs=2)
                 y_rows = result_of[group][:, t, 1:]
                 total = norm_of[group][:, t : t + 1]
                 if c >= VECTOR_SQUARES:
@@ -421,12 +364,11 @@ def tile_lorentzmultiheadattention_pb_t_kernel(
                         out=squares[:], in_=y_rows, func=ACT.Square, accum_out=total
                     )
 
-        def score_on_tensor(u):
-            if u not in TENSOR_SCORED:
+        def score_on_tensor(c, h):
+            if (c, h) not in TENSOR_SCORED:
                 return
-            c, h = UNITS[u]
             b, first, tiles = BLOCKS[c]
-            scores_of[u] = []
+            scores_of[c, h] = []
             for t in range(first, first + tiles):
                 scores_bank = psum.tile([P, SEQ], F32, tag="scores", bufs=2)
                 nc.tensor.matmul(
@@ -439,28 +381,27 @@ def tile_lorentzmultiheadattention_pb_t_kernel(
                 nc.tensor.matmul(
                     out=scores_bank[:],
                     lhsT=tq_rows[:, t:SEQ:ROW_TILES],
-                    rhs=tk_row_of[u][:],
+                    rhs=tk_row_of[c, h][:],
                     start=False,
                     stop=True,
                 )
-                scores_of[u].append(scores_bank[:])
+                scores_of[c, h].append(scores_bank[:])
 
-        def transpose_e(u):
-            e_bank_of[u] = transpose_rows(nc, psum, "e_bank", 2, identity[:], e_rows_of[u][:])
+        def transpose_e(c, h):
+            rows = e_rows_of[c, h][:]
+            e_bank_of[c, h] = transpose_rows(nc, psum, "e_bank", 2, identity[:], rows)
 
-        def transpose_wo(u):
+        def transpose_wo():
             wo_of["bank"] = transpose_rows(nc, psum, "e_bank", 2, identity[:], wo_rows[:])
 
-        def attend(u):
-            key, i, count = shared(u)
-            c, h = UNITS[u]
-            tiles = BLOCKS[c][2]
+        def attend(c, h):
+            b, first, tiles = BLOCKS[c]
             z_bank = psum.tile([P, tiles, HEAD_DIM], F32, tag="z")
             for a in range(tiles):
                 multiply(
-                    nc, z_bank[:, a, :], e_mx_of[key], i * tiles + a, v_mx_of[BLOCKS[c][0]], h * HEAD_DIM
+                    nc, z_bank[:, a, :], e_mx_of[c], h * tiles + a, v_mx_of[b], h * HEAD_DIM
                 )
-            z_of[u] = z_bank
+            z_of[c, h] = z_bank
 
         def transpose_m(c):
             m_bank_of[c] = transpose_rows(nc, psum, "m_bank", 1, identity[:], merged_of[c][:])
@@ -471,45 +412,59 @@ def tile_lorentzmultiheadattention_pb_t_kernel(
                 multiply(nc, y_bank[:, a, :], m_mx_of[c], a, wo_of["mx"], 0)
             y_of[c] = y_bank
 
-        def v_on_scalar(n):
-            return n < SCALAR_HEADS or n % HEADS == 0
+        def at(stage, c):
+            if 0 <= c < len(BLOCKS):
+                stage(c)
 
-        events = [(-1.6, prepare_tq, 0), (WO_TIMES[0], transpose_wo, 0), (WO_TIMES[1], regroup_wo, 0), (WO_TIMES[2], quantise_wo, 0)]
-        for stage, lag in [
-            (score_on_tensor, SCORE_ON_TENSOR),
-            (score_products, SCORE),
-            (score_maxima, MAXIMUM),
-            (score_shift, SHIFT),
-            (exponentiate, EXP),
-            (transpose_e, TRANSPOSE_E),
-            (regroup_e, REGROUP_E),
-            (quantise_e, QUANTISE_E),
-            (invert_rowsum, INVERT),
-            (attend, ATTEND),
-            (normalise, NORMALISE),
-        ]:
-            events.extend((UNIT_END[u] + lag, stage, u) for u in range(len(UNITS)))
-        for stage, lag in [
-            (transpose_m, TRANSPOSE_M),
-            (regroup_m, REGROUP_M),
-            (quantise_m, QUANTISE_M),
-            (project, PROJECT),
-            (add_bias, BIAS),
-            (sum_squares, SQUARES),
-            (finish, FINISH),
-        ]:
-            events.extend((BLOCK_END[c] + lag, stage, c) for c in range(len(BLOCKS)))
-        rooted = UNIT_END[-1] + NORMALISE + 0.05
-        events = [
-            (max(time, rooted), stage, c)
-            if stage == finish and rows_of_out(c)[0] == BATCH * ROW_TILES // GROUP_TILES - 1
-            else (time, stage, c)
-            for time, stage, c in events
-        ]
-        for n in range(ALL_HEADS):
-            t = max(FIRST_VALUES + n, HEADS * n + VALUES_ON_SCALAR) if v_on_scalar(n) else HEADS * n + VALUES_ON_VECTOR
-            events.append((t, regroup_values, n))
-            if n % 2:
-                events.append((t + QUANTISE_VALUES, quantise_values, n // 2))
-        for event in sorted(reversed(events), key=lambda event: event[0]):
-            event[1](event[2])
+        def at_head(stage, c, h):
+            if 0 <= c < len(BLOCKS):
+                stage(c, h)
+
+        def at_heads(stage, c):
+            for h in range(HEADS):
+                at_head(stage, c, h)
+
+        def starts_batch(c):
+            return 0 <= c < len(BLOCKS) and BLOCKS[c][1] == 0 and BLOCKS[c][0] >= 2
+
+        for c in range(len(BLOCKS) + 10):
+            at_head(transpose_e, c - 2, 0)
+            at_head(score_maxima, c - 1, 1)
+            at(quantise_m, c - 6)
+            at(project, c - 6)
+            at(regroup_m, c - 5)
+            at(score_shift, c - 1)
+            at_head(transpose_e, c - 2, 1)
+            at_heads(normalise, c - 4)
+            at(transpose_m, c - 4)
+            at_head(regroup_e, c - 2, 0)
+            if starts_batch(c - 2):
+                quantise_values(BLOCKS[c - 2][0])
+            at_head(score_products, c, 0)
+            at(sum_squares, c - 8)
+            at_head(exponentiate, c - 1, 0)
+            at(invert_rowsum, c - 2)
+            at(finish, c - 9)
+            at_head(exponentiate, c - 1, 1)
+            at_head(regroup_e, c - 2, 1)
+            at_head(score_products, c, 1)
+            at_head(score_on_tensor, c, 1)
+            at(quantise_e, c - 3)
+            at_head(score_on_tensor, c + 1, 0)
+            at(add_bias, c - 6)
+            at_head(score_maxima, c, 0)
+            if starts_batch(c):
+                regroup_values(BLOCKS[c][0], 1)
+            if starts_batch(c + 1):
+                regroup_values(BLOCKS[c + 1][0], 0)
+            if c == 1:
+                transpose_wo()
+                regroup_wo()
+            if c == 2:
+                quantise_wo()
+            if c in (2, 3):
+                for h in range(HEADS):
+                    regroup_values(c - 2, h)
+            if c in (3, 4):
+                quantise_values(c - 3)
+            at_heads(attend, c - 3)

@@ -12,6 +12,7 @@ ALU = mybir.AluOpType
 ACT = mybir.ActivationFunctionType
 
 P = 128
+QUADRANT = 32
 PACK = 4
 BATCH, HEADS, SEQ, HEAD_DIM, OUT_DIM = 8, 2, 512, 256, 256
 MODEL_DIM = HEADS * HEAD_DIM
@@ -28,7 +29,7 @@ BLOCKS = [
     for i in range(len(sizes))
 ]
 TENSOR_SCORED = ((1, 0), (1, 1), (4, 0), (8, 0), (12, 0), (17, 0))
-VECTOR_SQUARES = 8
+VECTOR_SQUARES = 9
 
 FLOPS = 2 * BATCH * HEADS * SEQ * SEQ * HEAD_DIM + 2 * BATCH * SEQ * MODEL_DIM * OUT_DIM
 
@@ -89,7 +90,12 @@ def tile_lorentzmultiheadattention_pb_t_kernel(
         psum = ctx.enter_context(tc.psum_pool(name="psum", bufs=2))
 
         tq_rows = const.tile([P, SEQ], BF16)
-        nc.vector.memset(tq_rows[:].bitcast(U32), 0)
+        for start in range(0, QUADRANT, ALL_HEADS):
+            nc.sync.dma_start(
+                out=tq_rows[start : start + ALL_HEADS, :], in_=tq.rearrange("b h i -> (b h) i")
+            )
+        nc.vector.memset(tq_rows[QUADRANT : 2 * QUADRANT, :].bitcast(U32), 0)
+        nc.vector.memset(tq_rows[2 * QUADRANT :, :].bitcast(U32), 0)
         tk_row_of = {}
 
         def make_tk_row(c, h):
@@ -137,7 +143,6 @@ def tile_lorentzmultiheadattention_pb_t_kernel(
             )
             v_tiles[b, h] = v_rows
 
-        nc.sync.dma_start(out=tq_rows[0:ALL_HEADS, :], in_=tq.rearrange("b h i -> (b h) i"))
         load_tk(0)
         for c, (b, first, tiles) in enumerate(BLOCKS):
             if b == 0:
@@ -432,11 +437,10 @@ def tile_lorentzmultiheadattention_pb_t_kernel(
             at_head(score_maxima, c - 1, 1)
             at(quantise_m, c - 6)
             at(project, c - 6)
-            at(regroup_m, c - 5)
             at(score_shift, c - 1)
             at_head(transpose_e, c - 2, 1)
             at_heads(normalise, c - 4)
-            at(transpose_m, c - 4)
+            at(regroup_m, c - 5)
             at_head(regroup_e, c - 2, 0)
             if starts_batch(c - 2):
                 quantise_values(BLOCKS[c - 2][0])
@@ -447,9 +451,9 @@ def tile_lorentzmultiheadattention_pb_t_kernel(
             at(finish, c - 9)
             at_head(exponentiate, c - 1, 1)
             at_head(regroup_e, c - 2, 1)
+            at(quantise_e, c - 3)
             at_head(score_products, c, 1)
             at_head(score_on_tensor, c, 1)
-            at(quantise_e, c - 3)
             at_head(score_on_tensor, c + 1, 0)
             at(add_bias, c - 6)
             at_head(score_maxima, c, 0)
@@ -468,3 +472,4 @@ def tile_lorentzmultiheadattention_pb_t_kernel(
             if c in (3, 4):
                 quantise_values(c - 3)
             at_heads(attend, c - 3)
+            at(transpose_m, c - 4)

from contextlib import ExitStack

import concourse.masks as masks
import concourse.mybir as mybir

F32 = mybir.dt.float32
BF16 = mybir.dt.bfloat16
U32 = mybir.dt.uint32
U8 = mybir.dt.uint8
FP8X4 = mybir.dt.float8_e4m3fn_x4
ALU = mybir.AluOpType
ACT = mybir.ActivationFunctionType

P = 128
QUADRANT = 32
PACK = 4
BATCH, HEADS, SEQ, HEAD_DIM, OUT_DIM = 8, 2, 512, 256, 256
MODEL_DIM = HEADS * HEAD_DIM
ROW_TILES = SEQ // P
ALL_HEADS = BATCH * HEADS
GROUP_TILES = 2 * ROW_TILES
INV_SCALE = 1.0 / 16.0

BLOCK_SIZES = {0: (1, 1, 2), BATCH - 1: (2, 1, 1)}
BLOCKS = [
    (b, sum(sizes[:i]), sizes[i])
    for b in range(BATCH)
    for sizes in [BLOCK_SIZES.get(b, (2, 2))]
    for i in range(len(sizes))
]
TENSOR_SCORED = ((1, 0), (1, 1), (4, 0), (8, 0), (12, 0), (17, 0))
VECTOR_SQUARES = 9

FLOPS = 2 * BATCH * HEADS * SEQ * SEQ * HEAD_DIM + 2 * BATCH * SEQ * MODEL_DIM * OUT_DIM


def transpose_rows(nc, psum, tag, bufs, identity, rows):
    tiles = rows.shape[1]
    bank = psum.tile([P, tiles, 2, P], F32, tag=tag, bufs=bufs)
    for a in range(tiles):
        words = rows[:, a, :].bitcast(F32)
        for u in range(2):
            nc.tensor.transpose(
                out=bank[:, a, u, :], in_=words[:, u : 2 * P : 2], identity=identity
            )
    return bank


def regroup(nc, grouped, bank):
    nc.scalar.copy(out=grouped.bitcast(F32), in_=bank[:].rearrange("p a u r -> p a r u"))


def quantise(nc, pool, grouped, name):
    words = grouped.shape[1] // PACK
    codes = pool.tile([P, words], U32, align_bytes=64, name=name + "_codes")
    scales = pool.tile([P, words], U8, align_bytes=64, name=name + "_scales")
    nc.vector.quantize_mx(out=codes[:].bitcast(FP8X4), scales=scales[:], in_=grouped)
    return codes, scales


def multiply(nc, product, rows, row_tile, columns, first_column):
    row_codes, row_scales = rows
    column_codes, column_scales = columns
    stationary = slice(row_tile * P, (row_tile + 1) * P)
    moving = slice(first_column, first_column + OUT_DIM)
    nc.tensor.matmul_mx(
        out=product,
        lhsT=row_codes[:, stationary].bitcast(FP8X4),
        lhsT_scale=row_scales[:, stationary],
        rhs=column_codes[:, moving].bitcast(FP8X4),
        rhs_scale=column_scales[:, moving],
        start=True,
        stop=True,
    )


def tile_lorentzmultiheadattention_pb_t_kernel(
    tc, qk_space, tq, tk, v_space, Wo, bo, out
):
    nc = tc.nc
    with ExitStack() as ctx:
        ctx.enter_context(tc.manual_schedule())
        const = ctx.enter_context(tc.tile_pool(name="const", bufs=1))
        inputs = ctx.enter_context(tc.tile_pool(name="inputs", bufs=ALL_HEADS))
        by_batch = ctx.enter_context(tc.tile_pool(name="by_batch", bufs=BATCH))
        work = ctx.enter_context(tc.tile_pool(name="work", bufs=4))
        kept = ctx.enter_context(tc.tile_pool(name="kept", bufs=10))
        groups = ctx.enter_context(tc.tile_pool(name="groups", bufs=3))
        values = ctx.enter_context(tc.tile_pool(name="values", bufs=3))
        psum = ctx.enter_context(tc.psum_pool(name="psum", bufs=2))

        tq_rows = const.tile([P, SEQ], BF16)
        for start in range(0, QUADRANT, ALL_HEADS):
            nc.sync.dma_start(
                out=tq_rows[start : start + ALL_HEADS, :], in_=tq.rearrange("b h i -> (b h) i")
            )
        nc.vector.memset(tq_rows[QUADRANT : 2 * QUADRANT, :].bitcast(U32), 0)
        nc.vector.memset(tq_rows[2 * QUADRANT :, :].bitcast(U32), 0)
        tk_row_of = {}

        def make_tk_row(c, h):
            tk_row = const.tile([P, SEQ], BF16, name="tk_row_%d_%d" % (c, h))
            nc.vector.memset(tk_row[:].bitcast(U32), 0)
            tk_row_of[c, h] = tk_row

        identity_bf16 = const.tile([P, P], BF16)
        masks.make_identity(nc, identity_bf16[:])
        identity = const.tile([P, P], F32)
        masks.make_identity(nc, identity[:])
        minus_identity = const.tile([P, P], BF16)
        nc.vector.tensor_scalar_mul(out=minus_identity[:], in0=identity_bf16[:], scalar1=-1.0)
        for c, h in TENSOR_SCORED:
            make_tk_row(c, h)
        half = const.tile([P, GROUP_TILES], F32)
        nc.gpsimd.memset(half[:], 0.5)

        qk_tiles, v_tiles, tk_tiles = {}, {}, {}
        wo_rows = const.tile([P, 2, MODEL_DIM], BF16)
        bias = const.tile([P, OUT_DIM], BF16)

        def load_tk(b):
            tk_all = by_batch.tile([P, HEADS, SEQ], BF16)
            nc.sync.dma_start(out=tk_all[:], in_=tk[b].partition_broadcast(P))
            tk_tiles[b] = tk_all

        def load_tk_row(c, h):
            b = BLOCKS[c][0]
            n = b * HEADS + h
            nc.sync.dma_start(out=tk_row_of[c, h][n : n + 1, :], in_=tk[b, h : h + 1])

        def load_qk(b, h, first, tiles):
            if first == 0:
                qk_rows = inputs.tile([P, ROW_TILES, SEQ], BF16)
                qk_tiles[b, h] = qk_rows
            rows = qk_space[b, h].rearrange("(p t) j -> p t j", t=ROW_TILES)
            span = slice(first, first + tiles)
            nc.sync.dma_start(out=qk_tiles[b, h][:, span, :], in_=rows[:, span, :])

        def load_v(b, h):
            v_rows = inputs.tile([P, PACK, HEAD_DIM], BF16)
            nc.sync.dma_start(
                out=v_rows[:], in_=v_space[b, h].rearrange("(p t) d -> p t d", t=PACK)
            )
            v_tiles[b, h] = v_rows

        load_tk(0)
        for c, (b, first, tiles) in enumerate(BLOCKS):
            if b == 0:
                for h in range(HEADS):
                    load_qk(b, h, first, tiles)
                if c == 0:
                    for h in range(HEADS):
                        load_tk_row(1, h)
                if c == 1:
                    nc.sync.dma_start(out=wo_rows[:], in_=Wo.rearrange("(a p) k -> p a k", p=P))
                    for h in range(HEADS):
                        load_v(0, h)
        nc.sync.dma_start(out=bias[:], in_=bo.partition_broadcast(P))
        for c, h in TENSOR_SCORED[HEADS:]:
            load_tk_row(c, h)
        for b in range(1, BATCH):
            load_tk(b)
            for h in range(HEADS):
                load_qk(b, h, 0, ROW_TILES)
            for h in range(HEADS):
                load_v(b, h)

        tq_columns = const.tile([P, ROW_TILES, ALL_HEADS], F32)

        tq_bank = psum.tile([P, ROW_TILES, P], BF16, tag="y", bufs=1)
        for t in range(ROW_TILES):
            nc.tensor.transpose(
                out=tq_bank[:, t, :], in_=tq_rows[:, t:SEQ:ROW_TILES], identity=identity_bf16[:]
            )
        nc.vector.tensor_copy(out=tq_columns[:], in_=tq_bank[:, :, 0:ALL_HEADS])

        v_grouped_of, v_mx_of, wo_of = {}, {}, {}
        scores_of, top_of, shift_of, e_rows_of, rowsum_of = {}, {}, {}, {}, {}
        e_bank_of, e_grouped_of, e_mx_of, inv_rowsum_of, z_of = {}, {}, {}, {}, {}
        merged_of, m_bank_of, m_grouped_of, m_mx_of = {}, {}, {}, {}
        y_of, result_of, norm_of = {}, {}, {}

        def rows_of_out(c):
            b, first, tiles = BLOCKS[c]
            group, place = divmod(b * ROW_TILES + first, GROUP_TILES)
            return group, range(place, place + tiles)

        def score_products(c, h):
            if (c, h) in TENSOR_SCORED:
                return
            b, first, tiles = BLOCKS[c]
            scores = work.tile([P, tiles, SEQ], F32)
            for a in range(tiles):
                nc.vector.scalar_tensor_tensor(
                    out=scores[:, a, :],
                    in0=tk_tiles[b][:, h, :],
                    scalar=tq_columns[:, first + a, b * HEADS + h : b * HEADS + h + 1],
                    in1=qk_tiles[b, h][:, first + a, :],
                    op0=ALU.mult,
                    op1=ALU.subtract,
                )
            scores_of[c, h] = [scores[:, a, :] for a in range(tiles)]

        def score_maxima(c, h):
            tiles = BLOCKS[c][2]
            if h == 0:
                top = kept.tile([P, HEADS, tiles], F32)
                top_of[c] = top
            for a in range(tiles):
                nc.vector.tensor_reduce(
                    out=top_of[c][:, h, a : a + 1],
                    in_=scores_of[c, h][a],
                    axis=mybir.AxisListType.X,
                    op=ALU.max,
                )

        def score_shift(c):
            shift = kept.tile([P, HEADS, BLOCKS[c][2]], F32)
            nc.vector.tensor_scalar_mul(out=shift[:], in0=top_of[c][:], scalar1=-INV_SCALE)
            shift_of[c] = shift

        def regroup_values(b, h):
            if h == 0:
                v_grouped = work.tile([P, HEADS, HEAD_DIM, PACK], BF16, align_bytes=64, bufs=2)
                v_grouped_of[b] = v_grouped
            copy = nc.vector.tensor_copy if b >= 2 and h == 1 else nc.scalar.copy
            copy(
                out=v_grouped_of[b][:, h].rearrange("p (c i) t -> p c t i", i=4),
                in_=v_tiles[b, h][:].rearrange("p t (c i) -> p c t i", i=4),
            )

        def quantise_values(b):
            v_mx_of[b] = quantise(
                nc, values, v_grouped_of[b][:].rearrange("p h d t -> p (h d t)"), "v"
            )

        def quantise_e(c):
            e_mx_of[c] = quantise(
                nc, work, e_grouped_of[c][:].rearrange("p h a r t -> p (h a r t)"), "e"
            )

        def invert_rowsum(c):
            inv_rowsum = kept.tile([P, HEADS, BLOCKS[c][2]], F32)
            nc.vector.reciprocal(out=inv_rowsum[:], in_=rowsum_of[c][:])
            inv_rowsum_of[c] = inv_rowsum

        def quantise_m(c):
            m_mx_of[c] = quantise(
                nc, work, m_grouped_of[c][:].rearrange("p a r t -> p (a r t)"), "m"
            )

        def quantise_wo():
            wo_of["mx"] = quantise(
                nc, const, wo_of["grouped"][:].rearrange("p a r t -> p (a r t)"), "wo"
            )

        def add_bias(c):
            group, place = rows_of_out(c)
            if place[0] == 0:
                result = groups.tile([P, GROUP_TILES, 1 + OUT_DIM], F32)
                norm = groups.tile([P, GROUP_TILES], F32)
                result_of[group], norm_of[group] = result, norm
            nc.vector.tensor_tensor(
                out=result_of[group][:, place[0] : place[-1] + 1, 1:],
                in0=y_of[c][:],
                in1=bias[:].unsqueeze(1).to_broadcast([P, len(place), OUT_DIM]),
                op=ALU.add,
            )

        def finish(c):
            group, place = rows_of_out(c)
            last_group = (group + 1) * GROUP_TILES == BATCH * ROW_TILES
            if last_group:
                span = slice(place[0], place[-1] + 1)
                nc.scalar.activation(
                    out=result_of[group][:, span, 0],
                    in_=norm_of[group][:, span],
                    func=ACT.Sqrt,
                    bias=1.0,
                )
                stores = [place]
            else:
                if place[-1] + 1 < GROUP_TILES:
                    return
                radicand = groups.tile([P, GROUP_TILES], F32)
                nc.gpsimd.tensor_scalar(
                    out=radicand[:],
                    in0=norm_of[group][:],
                    scalar1=1.0,
                    scalar2=None,
                    op0=ALU.add,
                )
                nc.gpsimd.tensor_tensor(
                    out=result_of[group][:, :, 0], in0=radicand[:], in1=half[:], op=ALU.pow
                )
                stores = [range(t, t + ROW_TILES) for t in range(0, GROUP_TILES, ROW_TILES)]
            for tiles in stores:
                b, t = divmod(group * GROUP_TILES + tiles[0], ROW_TILES)
                rows = out[b].rearrange("(p t) o -> p t o", t=ROW_TILES)
                nc.sync.dma_start(
                    out=rows[:, t : t + len(tiles), :],
                    in_=result_of[group][:, tiles[0] : tiles[-1] + 1, :],
                )

        def exponentiate(c, h):
            tiles = BLOCKS[c][2]
            e_rows = work.tile([P, tiles, SEQ], BF16)
            if h == 0:
                rowsum = kept.tile([P, HEADS, tiles], F32)
                rowsum_of[c] = rowsum
            for a in range(tiles):
                nc.scalar.activation(
                    out=e_rows[:, a, :],
                    in_=scores_of[c, h][a],
                    func=ACT.Exp,
                    bias=shift_of[c][:, h, a : a + 1],
                    scale=INV_SCALE,
                    accum_out=rowsum_of[c][:, h, a : a + 1],
                )
            e_rows_of[c, h] = e_rows

        def regroup_e(c, h):
            if h == 0:
                e_grouped = work.tile([P, HEADS, BLOCKS[c][2], P, PACK], BF16, align_bytes=64)
                e_grouped_of[c] = e_grouped
            regroup(nc, e_grouped_of[c][:, h], e_bank_of[c, h])

        def normalise(c, h):
            tiles = BLOCKS[c][2]
            if h == 0:
                merged = work.tile([P, tiles, MODEL_DIM], BF16, bufs=3)
                merged_of[c] = merged
            for a in range(tiles):
                nc.scalar.activation(
                    out=merged_of[c][:, a, h * HEAD_DIM : (h + 1) * HEAD_DIM],
                    in_=z_of[c, h][:, a, :],
                    func=ACT.Copy,
                    scale=inv_rowsum_of[c][:, h, a : a + 1],
                )

        def regroup_m(c):
            m_grouped = work.tile([P, BLOCKS[c][2], P, PACK], BF16, align_bytes=64, bufs=3)
            regroup(nc, m_grouped[:], m_bank_of[c])
            m_grouped_of[c] = m_grouped

        def regroup_wo():
            wo_grouped = const.tile([P, 2, P, PACK], BF16, align_bytes=64)
            regroup(nc, wo_grouped[:], wo_of["bank"])
            wo_of["grouped"] = wo_grouped

        def sum_squares(c):
            group, place = rows_of_out(c)
            for t in place:
                squares = work.tile([P, OUT_DIM], F32, bufs=2)
                y_rows = result_of[group][:, t, 1:]
                total = norm_of[group][:, t : t + 1]
                if c >= VECTOR_SQUARES:
                    nc.vector.scalar_tensor_tensor(
                        out=squares[:],
                        in0=y_rows,
                        scalar=1.0,
                        in1=y_rows,
                        op0=ALU.mult,
                        op1=ALU.mult,
                        accum_out=total,
                    )
                else:
                    nc.scalar.activation(
                        out=squares[:], in_=y_rows, func=ACT.Square, accum_out=total
                    )

        def score_on_tensor(c, h):
            if (c, h) not in TENSOR_SCORED:
                return
            b, first, tiles = BLOCKS[c]
            scores_of[c, h] = []
            for t in range(first, first + tiles):
                scores_bank = psum.tile([P, SEQ], F32, tag="scores", bufs=2)
                nc.tensor.matmul(
                    out=scores_bank[:],
                    lhsT=minus_identity[:],
                    rhs=qk_tiles[b, h][:, t, :],
                    start=True,
                    stop=False,
                )
                nc.tensor.matmul(
                    out=scores_bank[:],
                    lhsT=tq_rows[:, t:SEQ:ROW_TILES],
                    rhs=tk_row_of[c, h][:],
                    start=False,
                    stop=True,
                )
                scores_of[c, h].append(scores_bank[:])

        def transpose_e(c, h):
            rows = e_rows_of[c, h][:]
            e_bank_of[c, h] = transpose_rows(nc, psum, "e_bank", 2, identity[:], rows)

        def transpose_wo():
            wo_of["bank"] = transpose_rows(nc, psum, "e_bank", 2, identity[:], wo_rows[:])

        def attend(c, h):
            b, first, tiles = BLOCKS[c]
            z_bank = psum.tile([P, tiles, HEAD_DIM], F32, tag="z")
            for a in range(tiles):
                multiply(
                    nc, z_bank[:, a, :], e_mx_of[c], h * tiles + a, v_mx_of[b], h * HEAD_DIM
                )
            z_of[c, h] = z_bank

        def transpose_m(c):
            m_bank_of[c] = transpose_rows(nc, psum, "m_bank", 1, identity[:], merged_of[c][:])

        def project(c):
            y_bank = psum.tile([P, BLOCKS[c][2], OUT_DIM], F32, tag="y", bufs=1)
            for a in range(BLOCKS[c][2]):
                multiply(nc, y_bank[:, a, :], m_mx_of[c], a, wo_of["mx"], 0)
            y_of[c] = y_bank

        def at(stage, c):
            if 0 <= c < len(BLOCKS):
                stage(c)

        def at_head(stage, c, h):
            if 0 <= c < len(BLOCKS):
                stage(c, h)

        def at_heads(stage, c):
            for h in range(HEADS):
                at_head(stage, c, h)

        def starts_batch(c):
            return 0 <= c < len(BLOCKS) and BLOCKS[c][1] == 0 and BLOCKS[c][0] >= 2

        for c in range(len(BLOCKS) + 10):
            at_head(transpose_e, c - 2, 0)
            at_head(score_maxima, c - 1, 1)
            at(quantise_m, c - 6)
            at(project, c - 6)
            at(score_shift, c - 1)
            at_head(transpose_e, c - 2, 1)
            at_heads(normalise, c - 4)
            at(regroup_m, c - 5)
            at_head(regroup_e, c - 2, 0)
            if starts_batch(c - 2):
                quantise_values(BLOCKS[c - 2][0])
            at_head(score_products, c, 0)
            at(sum_squares, c - 8)
            at_head(exponentiate, c - 1, 0)
            at(invert_rowsum, c - 2)
            at(finish, c - 9)
            at_head(exponentiate, c - 1, 1)
            at_head(regroup_e, c - 2, 1)
            at(quantise_e, c - 3)
            at_head(score_products, c, 1)
            at_head(score_on_tensor, c, 1)
            at_head(score_on_tensor, c + 1, 0)
            at(add_bias, c - 6)
            at_head(score_maxima, c, 0)
            if starts_batch(c):
                regroup_values(BLOCKS[c][0], 1)
            if starts_batch(c + 1):
                regroup_values(BLOCKS[c + 1][0], 0)
            if c == 1:
                transpose_wo()
                regroup_wo()
            if c == 2:
                quantise_wo()
            if c in (2, 3):
                for h in range(HEADS):
                    regroup_values(c - 2, h)
            if c in (3, 4):
                quantise_values(c - 3)
            at_heads(attend, c - 3)
            at(transpose_m, c - 4)
